import numpy as np
import ml_dtypes


def mxq(x, axis, fmt="e4m3"):
    dtype, down = {"e4m3": (ml_dtypes.float8_e4m3fn, 7), "e5m2": (ml_dtypes.float8_e5m2, 14)}[fmt]
    v = np.moveaxis(np.asarray(x, np.float32).astype(ml_dtypes.bfloat16).astype(np.float64), axis, -1)
    blocks = v.reshape(v.shape[:-1] + (-1, 32))
    amax = np.abs(blocks).max(-1, keepdims=True)
    byte = np.maximum(np.where(amax > 0, np.frexp(amax)[1] - 1 + 127, 0) - down, 1)
    scale = np.exp2(byte - 127.0)
    codes = (blocks / scale).astype(np.float32).astype(dtype).astype(np.float64)
    return np.moveaxis((codes * scale).reshape(v.shape), -1, axis)


WIDE = False


def mx_kscale(k):
    if not WIDE:
        return np.ones(k)
    levels = np.array([10, -10, 5, -5, 0])
    a = np.random.permutation(np.resize(levels, k // 512 * 4)).reshape(k // 512, 4)
    idx = np.arange(k)
    return np.exp2(a[idx // 512, idx % 128 // 32])


BF16 = ml_dtypes.bfloat16


def bf(x):
    return np.asarray(x, np.float32).astype(BF16)


def f64(x):
    return np.asarray(x).astype(np.float64)


B, H, E, V = 512, 1024, 1024, 4096


def sigmoid(v):
    return 1.0 / (1.0 + np.exp(-v))


def setup_inputs():
    s, t = mx_kscale(E), mx_kscale(H)
    return {
        "input_data": bf(np.random.standard_normal((B, E)) * s),
        "previous_hidden_state": bf(np.random.standard_normal((B, H)) * t),
        "c_t": bf(np.random.standard_normal((B, H)) * 0.7),
        "w_ip_o": bf(np.random.standard_normal((E, H)) / np.sqrt(E) / s[:, None]),
        "w_output": bf(np.random.standard_normal((H, H)) / np.sqrt(H) / t[:, None]),
        "w_output_c": bf(np.random.standard_normal((H, H)) / np.sqrt(H)),
        "w_op": bf(np.random.standard_normal((H, V)) * 3.0 / np.sqrt(H)),
    }


def reference(input_data, previous_hidden_state, c_t, w_ip_o, w_output, w_output_c, w_op):
    ct = f64(c_t)
    zo = (mxq(f64(input_data), 1, "e4m3") @ mxq(f64(w_ip_o), 0, "e4m3")) \
        + (mxq(f64(previous_hidden_state), 1, "e4m3") @ mxq(f64(w_output), 0, "e4m3"))
    ot = sigmoid(zo + (mxq(ct, 1, "e4m3") @ mxq(f64(w_output_c), 0, "e4m3")))
    ht = ot * np.tanh(ct)
    yt = sigmoid(mxq(ht, 1, "e4m3") @ mxq(f64(w_op), 0, "e4m3"))
    return yt, ht

@@ -1,0 +1,235 @@
+from contextlib import ExitStack
+
+import concourse.mybir as mybir
+from concourse.masks import make_identity
+
+F32 = mybir.dt.float32
+BF16 = mybir.dt.bfloat16
+U32 = mybir.dt.uint32
+U8 = mybir.dt.uint8
+FP8X4 = mybir.dt.float8_e4m3fn_x4
+ACT = mybir.ActivationFunctionType
+
+P = 128
+PACK = 4
+K_PASS = P * PACK
+BATCH = 512
+HIDDEN = 1024
+VOCAB = 4096
+B_TILES = BATCH // P
+PASSES = HIDDEN // K_PASS
+N_TILE = 512
+CHUNK_COLS = 1024
+CHUNK_ELEMS = PACK * CHUNK_COLS
+HALVES = CHUNK_COLS // N_TILE
+RUN = 4
+
+N_ACTS = 3
+GATE_CHUNKS = N_ACTS * PASSES
+READOUT_BLOCKS = VOCAB // CHUNK_COLS
+WEIGHT_CHUNKS = GATE_CHUNKS + READOUT_BLOCKS * PASSES
+
+GATE_VECTOR_COLS = 512
+READOUT_VECTOR_COLS = 832
+
+RAW_BUFS = 10
+
+FLOPS = 2 * BATCH * HIDDEN * (N_ACTS * HIDDEN + VOCAB)
+
+
+def tile_lstm_peephole_build_pb_kernel(
+    tc, input_data, previous_hidden_state, c_t, w_ip_o, w_output, w_output_c, w_op, out_0, out_1
+):
+    nc = tc.nc
+    yt_rows = out_0.rearrange("(p i) n -> p i n", i=B_TILES)
+    ht_rows = out_1.rearrange("(p i) n -> p i n", i=B_TILES)
+
+    sources = []
+    for act in (input_data, previous_hidden_state, c_t):
+        sources.append(act.rearrange("(p i) k -> p i k", i=B_TILES))
+    for weight in (w_ip_o, w_output, w_output_c):
+        for g in range(PASSES):
+            rows = weight[g * K_PASS : (g + 1) * K_PASS, :]
+            sources.append(rows.rearrange("(u q e) n -> q u (e n)", u=2, e=2))
+    for block in range(READOUT_BLOCKS):
+        for g in range(PASSES):
+            rows = w_op[
+                g * K_PASS : (g + 1) * K_PASS, block * CHUNK_COLS : (block + 1) * CHUNK_COLS
+            ]
+            sources.append(rows.rearrange("(t p) n -> p t n", p=P))
+
+    with ExitStack() as ctx:
+        const = ctx.enter_context(tc.tile_pool(name="const", bufs=1))
+        keep = ctx.enter_context(tc.tile_pool(name="keep", bufs=1))
+        raw_pool = ctx.enter_context(tc.tile_pool(name="raw", bufs=RAW_BUFS))
+        grouped_pool = ctx.enter_context(tc.tile_pool(name="grouped", bufs=4))
+        codes_pool = ctx.enter_context(tc.tile_pool(name="codes", bufs=6))
+        sig_pool = ctx.enter_context(tc.tile_pool(name="sig", bufs=3))
+        y_pool = ctx.enter_context(tc.tile_pool(name="y", bufs=6))
+        psum = ctx.enter_context(tc.psum_pool(name="psum", bufs=8))
+
+        raws = {}
+
+        def load(j):
+            if j < len(sources):
+                raw = raw_pool.tile([P, CHUNK_ELEMS], BF16, tag="raw")
+                nc.sync.dma_start(
+                    out=raw[:].rearrange("p (r m) -> p r m", r=sources[j].shape[1]),
+                    in_=sources[j],
+                )
+                raws[j] = raw
+
+        for j in range(RAW_BUFS):
+            load(j)
+
+        ident = const.tile([P, P], F32)
+        make_identity(nc, ident[:])
+
+        warm = const.tile([P, 1], F32)
+        nc.vector.memset(warm[:], 0.0)
+        nc.scalar.activation(out=warm[:], in_=warm[:], func=ACT.Sigmoid)
+
+        act_codes = keep.tile([P, N_ACTS, B_TILES * PASSES * P], U32, align_bytes=64)
+        act_scales = keep.tile([P, N_ACTS, B_TILES * PASSES * P], U8, align_bytes=64)
+        tanh_c = keep.tile([P, B_TILES, HIDDEN], F32)
+
+        for a in range(N_ACTS):
+            words = raws[a][:].bitcast(F32)
+            grouped = grouped_pool.tile([P, CHUNK_ELEMS], BF16, tag="grouped", align_bytes=64)
+            grouped_words = grouped[:].bitcast(F32)
+            words_per_tile = HIDDEN // 2
+            for i in range(B_TILES):
+                bank = psum.tile([P, PASSES * 2, P], F32, tag="bank")
+                for w in range(PASSES * 2):
+                    first = i * words_per_tile + w * P
+                    nc.tensor.transpose(bank[:, w, :], words[:, first : first + P], ident[:])
+                dst = grouped_words[:, i * words_per_tile : (i + 1) * words_per_tile]
+                dst = dst.rearrange("p (g b u) -> p g b u", g=PASSES, u=2)
+                src = bank[:].rearrange("p (g u) b -> p g b u", u=2)
+                if i % 2 == 0:
+                    nc.scalar.copy(out=dst, in_=src)
+                else:
+                    nc.vector.tensor_copy(out=dst, in_=src)
+            nc.vector.quantize_mx(
+                out=act_codes[:, a, :].bitcast(FP8X4), scales=act_scales[:, a, :], in_=grouped[:]
+            )
+            if a == N_ACTS - 1:
+                for i in range(B_TILES):
+                    nc.scalar.activation(
+                        out=tanh_c[:, i, :],
+                        in_=raws[a][:, i * HIDDEN : (i + 1) * HIDDEN],
+                        func=ACT.Tanh,
+                    )
+            load(a + RAW_BUFS)
+
+        grouped_of = {}
+        codes_of = {}
+        scales_of = {}
+
+        def regroup(j):
+            raw = raws[N_ACTS + j]
+            grouped = grouped_pool.tile([P, CHUNK_ELEMS], BF16, tag="grouped", align_bytes=64)
+            src = raw[:].rearrange("p (t c r) -> p c t r", t=PACK, r=RUN)
+            dst = grouped[:].rearrange("p (c r t) -> p c t r", r=RUN, t=PACK)
+            vector_cols = GATE_VECTOR_COLS if j < GATE_CHUNKS else READOUT_VECTOR_COLS
+            split = vector_cols // RUN
+            nc.vector.tensor_copy(out=dst[:, :split, :, :], in_=src[:, :split, :, :])
+            nc.scalar.copy(out=dst[:, split:, :, :], in_=src[:, split:, :, :])
+            grouped_of[j] = grouped
+            load(N_ACTS + j + RAW_BUFS)
+
+        def quantise(j):
+            codes = codes_pool.tile([P, CHUNK_COLS], U32, tag="codes", align_bytes=64)
+            scales = codes_pool.tile([P, CHUNK_COLS], U8, tag="scales", align_bytes=64)
+            nc.vector.quantize_mx(
+                out=codes[:].bitcast(FP8X4), scales=scales[:], in_=grouped_of[j][:]
+            )
+            codes_of[j] = codes
+            scales_of[j] = scales
+
+        zo = {}
+
+        def gate_passes(j):
+            a, g = divmod(j, PASSES)
+            for half in range(HALVES):
+                cols = slice(half * N_TILE, (half + 1) * N_TILE)
+                for i in range(B_TILES):
+                    if j == 0:
+                        zo[(i, half)] = psum.tile([P, N_TILE], F32, tag="bank", name="zo")
+                    rows = slice((i * PASSES + g) * P, (i * PASSES + g + 1) * P)
+                    nc.tensor.matmul_mx(
+                        out=zo[(i, half)][:],
+                        lhsT=act_codes[:, a, rows].bitcast(FP8X4),
+                        lhsT_scale=act_scales[:, a, rows],
+                        rhs=codes_of[j][:, cols].bitcast(FP8X4),
+                        rhs_scale=scales_of[j][:, cols],
+                        start=(j == 0),
+                        stop=(j == GATE_CHUNKS - 1),
+                    )
+
+        ht_grouped = keep.tile([P, PASSES, B_TILES * P * PACK], BF16, align_bytes=64)
+        ht_codes = keep.tile([P, PASSES, B_TILES * P], U32, align_bytes=64)
+        ht_scales = keep.tile([P, PASSES, B_TILES * P], U8, align_bytes=64)
+
+        def gate_epilogue():
+            for g in range(PASSES):
+                for i in range(B_TILES):
+                    sig = sig_pool.tile([P, N_TILE], F32, tag="sig")
+                    nc.scalar.activation(out=sig[:], in_=zo[(i, g)][:], func=ACT.Sigmoid)
+                    ht = tanh_c[:, i, g * K_PASS : (g + 1) * K_PASS]
+                    nc.vector.tensor_mul(out=ht, in0=sig[:], in1=ht)
+                    bank = psum.tile([P, PACK, P], F32, tag="bank")
+                    for t in range(PACK):
+                        nc.tensor.transpose(bank[:, t, :], ht[:, t * P : (t + 1) * P], ident[:])
+                    dst = ht_grouped[:, g, i * K_PASS : (i + 1) * K_PASS]
+                    dst = dst.rearrange("p (b t) -> p b t", t=PACK)
+                    src = bank[:].rearrange("p t b -> p b t")
+                    if i % 2 == 0:
+                        nc.scalar.copy(out=dst, in_=src)
+                    else:
+                        nc.vector.tensor_copy(out=dst, in_=src)
+                nc.vector.quantize_mx(
+                    out=ht_codes[:, g, :].bitcast(FP8X4),
+                    scales=ht_scales[:, g, :],
+                    in_=ht_grouped[:, g, :],
+                )
+            for i in range(B_TILES):
+                nc.sync.dma_start(out=ht_rows[:, i, :], in_=tanh_c[:, i, :])
+
+        def readout_block(block):
+            first = GATE_CHUNKS + block * PASSES
+            for i in range(B_TILES):
+                y = y_pool.tile([P, CHUNK_COLS], F32, tag="y")
+                rows = slice(i * P, (i + 1) * P)
+                for half in range(HALVES):
+                    cols = slice(half * N_TILE, (half + 1) * N_TILE)
+                    acc = psum.tile([P, N_TILE], F32, tag="bank")
+                    for g in range(PASSES):
+                        nc.tensor.matmul_mx(
+                            out=acc[:],
+                            lhsT=ht_codes[:, g, rows].bitcast(FP8X4),
+                            lhsT_scale=ht_scales[:, g, rows],
+                            rhs=codes_of[first + g][:, cols].bitcast(FP8X4),
+                            rhs_scale=scales_of[first + g][:, cols],
+                            start=(g == 0),
+                            stop=(g == PASSES - 1),
+                        )
+                    nc.scalar.activation(out=y[:, cols], in_=acc[:], func=ACT.Sigmoid)
+                nc.sync.dma_start(
+                    out=yt_rows[:, i, block * CHUNK_COLS : (block + 1) * CHUNK_COLS], in_=y[:]
+                )
+
+        def finish(j):
+            quantise(j)
+            if j < GATE_CHUNKS:
+                gate_passes(j)
+                if j == GATE_CHUNKS - 1:
+                    gate_epilogue()
+            elif (j - GATE_CHUNKS) % PASSES == PASSES - 1:
+                readout_block((j - GATE_CHUNKS) // PASSES)
+
+        for j in range(WEIGHT_CHUNKS):
+            regroup(j)
+            if j > 0:
+                finish(j - 1)
+        finish(WEIGHT_CHUNKS - 1)

@@ -27,12 +27,19 @@ RUN = 4
 N_ACTS = 3
 GATE_CHUNKS = N_ACTS * PASSES
 READOUT_BLOCKS = VOCAB // CHUNK_COLS
-WEIGHT_CHUNKS = GATE_CHUNKS + READOUT_BLOCKS * PASSES
 
-GATE_VECTOR_COLS = 512
-READOUT_VECTOR_COLS = 832
+N_BLOCKS = VOCAB // N_TILE
+UNITS = GATE_CHUNKS + N_BLOCKS
 
-RAW_BUFS = 10
+BANK_COLS = 256
+GATE_TENSOR_COLS = 512
+READOUT_TENSOR_COLS = 256
+
+SUM_BANKS = 6
+SPARE_BANKS = 2
+EARLY_TILES = SUM_BANKS // HALVES
+
+RAW_BUFS = 8
 
 FLOPS = 2 * BATCH * HIDDEN * (N_ACTS * HIDDEN + VOCAB)
 
@@ -63,27 +70,39 @@ def tile_lstm_peephole_build_pb_kernel(
         keep = ctx.enter_context(tc.tile_pool(name="keep", bufs=1))
         raw_pool = ctx.enter_context(tc.tile_pool(name="raw", bufs=RAW_BUFS))
         grouped_pool = ctx.enter_context(tc.tile_pool(name="grouped", bufs=4))
-        codes_pool = ctx.enter_context(tc.tile_pool(name="codes", bufs=6))
+        gate_codes_pool = ctx.enter_context(tc.tile_pool(name="gate_codes", bufs=GATE_CHUNKS))
+        codes_pool = ctx.enter_context(tc.tile_pool(name="codes", bufs=4))
         sig_pool = ctx.enter_context(tc.tile_pool(name="sig", bufs=3))
         y_pool = ctx.enter_context(tc.tile_pool(name="y", bufs=6))
-        psum = ctx.enter_context(tc.psum_pool(name="psum", bufs=8))
+        sums = ctx.enter_context(tc.psum_pool(name="sums", bufs=SUM_BANKS))
+        spare = ctx.enter_context(tc.psum_pool(name="spare", bufs=SPARE_BANKS))
 
         raws = {}
 
         def load(j):
             if j < len(sources):
                 raw = raw_pool.tile([P, CHUNK_ELEMS], BF16, tag="raw")
-                nc.sync.dma_start(
-                    out=raw[:].rearrange("p (r m) -> p r m", r=sources[j].shape[1]),
-                    in_=sources[j],
-                )
+                runs = sources[j].shape[1]
+                dst = raw[:].rearrange("p (r m) -> p r m", r=runs)
+                pieces = runs if j == 0 else 1
+                step = runs // pieces
+                for r in range(0, runs, step):
+                    nc.sync.dma_start(out=dst[:, r : r + step, :], in_=sources[j][:, r : r + step, :])
                 raws[j] = raw
 
+        loaded = []
+
+        def load_next():
+            load(len(loaded))
+            loaded.append(True)
+
         for j in range(RAW_BUFS):
-            load(j)
+            load_next()
 
         ident = const.tile([P, P], F32)
         make_identity(nc, ident[:])
+        ident_bf = const.tile([P, P], BF16)
+        make_identity(nc, ident_bf[:])
 
         warm = const.tile([P, 1], F32)
         nc.vector.memset(warm[:], 0.0)
@@ -99,7 +118,7 @@ def tile_lstm_peephole_build_pb_kernel(
             grouped_words = grouped[:].bitcast(F32)
             words_per_tile = HIDDEN // 2
             for i in range(B_TILES):
-                bank = psum.tile([P, PASSES * 2, P], F32, tag="bank")
+                bank = spare.tile([P, PASSES * 2, P], F32, tag="bank")
                 for w in range(PASSES * 2):
                     first = i * words_per_tile + w * P
                     nc.tensor.transpose(bank[:, w, :], words[:, first : first + P], ident[:])
@@ -113,123 +132,183 @@ def tile_lstm_peephole_build_pb_kernel(
             nc.vector.quantize_mx(
                 out=act_codes[:, a, :].bitcast(FP8X4), scales=act_scales[:, a, :], in_=grouped[:]
             )
-            if a == N_ACTS - 1:
-                for i in range(B_TILES):
-                    nc.scalar.activation(
-                        out=tanh_c[:, i, :],
-                        in_=raws[a][:, i * HIDDEN : (i + 1) * HIDDEN],
-                        func=ACT.Tanh,
-                    )
-            load(a + RAW_BUFS)
+            if a < N_ACTS - 1:
+                load_next()
+
+        def tanh_tile(i):
+            nc.scalar.activation(
+                out=tanh_c[:, i, :],
+                in_=raws[N_ACTS - 1][:, i * HIDDEN : (i + 1) * HIDDEN],
+                func=ACT.Tanh,
+            )
+            if i == B_TILES - 1:
+                load_next()
+
+        def parts_of(unit):
+            if unit < GATE_CHUNKS:
+                return [(N_ACTS + unit, 0), (N_ACTS + unit, N_TILE)]
+            block, half = divmod(unit - GATE_CHUNKS, HALVES)
+            first = N_ACTS + GATE_CHUNKS + block * PASSES
+            return [(first + g, half * N_TILE) for g in range(PASSES)]
 
         grouped_of = {}
         codes_of = {}
         scales_of = {}
 
-        def regroup(j):
-            raw = raws[N_ACTS + j]
+        def regroup(unit):
             grouped = grouped_pool.tile([P, CHUNK_ELEMS], BF16, tag="grouped", align_bytes=64)
-            src = raw[:].rearrange("p (t c r) -> p c t r", t=PACK, r=RUN)
-            dst = grouped[:].rearrange("p (c r t) -> p c t r", r=RUN, t=PACK)
-            vector_cols = GATE_VECTOR_COLS if j < GATE_CHUNKS else READOUT_VECTOR_COLS
-            split = vector_cols // RUN
-            nc.vector.tensor_copy(out=dst[:, :split, :, :], in_=src[:, :split, :, :])
-            nc.scalar.copy(out=dst[:, split:, :, :], in_=src[:, split:, :, :])
-            grouped_of[j] = grouped
-            load(N_ACTS + j + RAW_BUFS)
+            dst = grouped[:].rearrange("p (s c r t) -> p s c t r", s=2, r=RUN, t=PACK)
+            tensor_cols = GATE_TENSOR_COLS if unit < GATE_CHUNKS else READOUT_TENSOR_COLS
+            vector_cols = N_TILE - tensor_cols
+            for s, (j, col) in enumerate(parts_of(unit)):
+                src = raws[j][:].rearrange("p (t c r) -> p c t r", t=PACK, r=RUN)
+                src = src[:, col // RUN : (col + N_TILE) // RUN, :, :]
+                if s == 0:
+                    nc.vector.tensor_copy(out=dst[:, s, :, :, :], in_=src)
+                    continue
+                if vector_cols > 0:
+                    split = vector_cols // RUN
+                    nc.vector.tensor_copy(out=dst[:, s, :split, :, :], in_=src[:, :split, :, :])
+                rows = raws[j][:].rearrange("p (t n) -> p t n", t=PACK)
+                for first in range(vector_cols, N_TILE, BANK_COLS):
+                    bank = spare.tile([P, BANK_COLS, PACK], BF16, tag="bank")
+                    for n in range(0, BANK_COLS, P):
+                        nc.tensor.matmul(
+                            out=bank[:, n : n + P, :].rearrange("p n t -> p t n"),
+                            lhsT=ident_bf[:],
+                            rhs=rows[:, :, col + first + n : col + first + n + P],
+                            start=True,
+                            stop=True,
+                        )
+                    place = (N_TILE + first) * PACK
+                    nc.scalar.copy(
+                        out=grouped[:, place : place + BANK_COLS * PACK],
+                        in_=bank[:].rearrange("p n t -> p (n t)"),
+                    )
+            grouped_of[unit] = grouped
+            if unit < GATE_CHUNKS:
+                load_next()
+            elif (unit - GATE_CHUNKS) % HALVES == HALVES - 1:
+                for g in range(PASSES):
+                    load_next()
 
-        def quantise(j):
-            codes = codes_pool.tile([P, CHUNK_COLS], U32, tag="codes", align_bytes=64)
-            scales = codes_pool.tile([P, CHUNK_COLS], U8, tag="scales", align_bytes=64)
+        def quantise(unit):
+            pool = gate_codes_pool if unit < GATE_CHUNKS else codes_pool
+            codes = pool.tile([P, 2, N_TILE], U32, tag="codes", align_bytes=64)
+            scales = pool.tile([P, 2, N_TILE], U8, tag="scales", align_bytes=64)
             nc.vector.quantize_mx(
-                out=codes[:].bitcast(FP8X4), scales=scales[:], in_=grouped_of[j][:]
+                out=codes[:].rearrange("p s n -> p (s n)").bitcast(FP8X4),
+                scales=scales[:].rearrange("p s n -> p (s n)"),
+                in_=grouped_of[unit][:],
             )
-            codes_of[j] = codes
-            scales_of[j] = scales
+            codes_of[unit] = codes
+            scales_of[unit] = scales
 
         zo = {}
 
-        def gate_passes(j):
+        def gate_pass(j, i, half):
             a, g = divmod(j, PASSES)
+            if j == 0:
+                zo[(i, half)] = sums.tile([P, N_TILE], F32, tag="sum", name="zo")
+            rows = slice((i * PASSES + g) * P, (i * PASSES + g + 1) * P)
+            nc.tensor.matmul_mx(
+                out=zo[(i, half)][:],
+                lhsT=act_codes[:, a, rows].bitcast(FP8X4),
+                lhsT_scale=act_scales[:, a, rows],
+                rhs=codes_of[j][:, half, :].bitcast(FP8X4),
+                rhs_scale=scales_of[j][:, half, :],
+                start=(j == 0),
+                stop=(j == GATE_CHUNKS - 1),
+            )
+
+        ht_grouped = keep.tile([P, B_TILES, PASSES * P * PACK], BF16, align_bytes=64)
+        ht_codes = keep.tile([P, B_TILES, PASSES * P], U32, align_bytes=64)
+        ht_scales = keep.tile([P, B_TILES, PASSES * P], U8, align_bytes=64)
+
+        def hidden_state(i):
+            sig = sig_pool.tile([P, HIDDEN], F32, tag="sig")
             for half in range(HALVES):
-                cols = slice(half * N_TILE, (half + 1) * N_TILE)
-                for i in range(B_TILES):
-                    if j == 0:
-                        zo[(i, half)] = psum.tile([P, N_TILE], F32, tag="bank", name="zo")
-                    rows = slice((i * PASSES + g) * P, (i * PASSES + g + 1) * P)
+                nc.scalar.activation(
+                    out=sig[:, half * N_TILE : (half + 1) * N_TILE],
+                    in_=zo[(i, half)][:],
+                    func=ACT.Sigmoid,
+                )
+            nc.vector.tensor_mul(out=tanh_c[:, i, :], in0=sig[:], in1=tanh_c[:, i, :])
+            nc.sync.dma_start(out=ht_rows[:, i, :], in_=tanh_c[:, i, :])
+
+        def quantise_hidden_state(i):
+            for g in range(PASSES):
+                bank = spare.tile([P, PACK, P], F32, tag="bank")
+                for t in range(PACK):
+                    first = g * K_PASS + t * P
+                    nc.tensor.transpose(bank[:, t, :], tanh_c[:, i, first : first + P], ident[:])
+                dst = ht_grouped[:, i, g * K_PASS : (g + 1) * K_PASS]
+                nc.scalar.copy(
+                    out=dst.rearrange("p (b t) -> p b t", t=PACK),
+                    in_=bank[:].rearrange("p t b -> p b t"),
+                )
+            nc.vector.quantize_mx(
+                out=ht_codes[:, i, :].bitcast(FP8X4),
+                scales=ht_scales[:, i, :],
+                in_=ht_grouped[:, i, :],
+            )
+
+        y_of = {}
+
+        def readout_passes(unit):
+            block, half = divmod(unit - GATE_CHUNKS, HALVES)
+            for i in range(B_TILES):
+                if half == 0:
+                    y_of[i] = y_pool.tile([P, CHUNK_COLS], F32, tag="y", name="y")
+                acc = sums.tile([P, N_TILE], F32, tag="sum")
+                for g in range(PASSES):
+                    rows = slice(g * P, (g + 1) * P)
                     nc.tensor.matmul_mx(
-                        out=zo[(i, half)][:],
-                        lhsT=act_codes[:, a, rows].bitcast(FP8X4),
-                        lhsT_scale=act_scales[:, a, rows],
-                        rhs=codes_of[j][:, cols].bitcast(FP8X4),
-                        rhs_scale=scales_of[j][:, cols],
-                        start=(j == 0),
-                        stop=(j == GATE_CHUNKS - 1),
+                        out=acc[:],
+                        lhsT=ht_codes[:, i, rows].bitcast(FP8X4),
+                        lhsT_scale=ht_scales[:, i, rows],
+                        rhs=codes_of[unit][:, g, :].bitcast(FP8X4),
+                        rhs_scale=scales_of[unit][:, g, :],
+                        start=(g == 0),
+                        stop=(g == PASSES - 1),
+                    )
+                nc.scalar.activation(
+                    out=y_of[i][:, half * N_TILE : (half + 1) * N_TILE], in_=acc[:], func=ACT.Sigmoid
+                )
+                if half == HALVES - 1:
+                    nc.sync.dma_start(
+                        out=yt_rows[:, i, block * CHUNK_COLS : (block + 1) * CHUNK_COLS],
+                        in_=y_of[i][:],
                     )
 
-        ht_grouped = keep.tile([P, PASSES, B_TILES * P * PACK], BF16, align_bytes=64)
-        ht_codes = keep.tile([P, PASSES, B_TILES * P], U32, align_bytes=64)
-        ht_scales = keep.tile([P, PASSES, B_TILES * P], U8, align_bytes=64)
-
-        def gate_epilogue():
-            for g in range(PASSES):
-                for i in range(B_TILES):
-                    sig = sig_pool.tile([P, N_TILE], F32, tag="sig")
-                    nc.scalar.activation(out=sig[:], in_=zo[(i, g)][:], func=ACT.Sigmoid)
-                    ht = tanh_c[:, i, g * K_PASS : (g + 1) * K_PASS]
-                    nc.vector.tensor_mul(out=ht, in0=sig[:], in1=ht)
-                    bank = psum.tile([P, PACK, P], F32, tag="bank")
-                    for t in range(PACK):
-                        nc.tensor.transpose(bank[:, t, :], ht[:, t * P : (t + 1) * P], ident[:])
-                    dst = ht_grouped[:, g, i * K_PASS : (i + 1) * K_PASS]
-                    dst = dst.rearrange("p (b t) -> p b t", t=PACK)
-                    src = bank[:].rearrange("p t b -> p b t")
-                    if i % 2 == 0:
-                        nc.scalar.copy(out=dst, in_=src)
-                    else:
-                        nc.vector.tensor_copy(out=dst, in_=src)
-                nc.vector.quantize_mx(
-                    out=ht_codes[:, g, :].bitcast(FP8X4),
-                    scales=ht_scales[:, g, :],
-                    in_=ht_grouped[:, g, :],
-                )
-            for i in range(B_TILES):
-                nc.sync.dma_start(out=ht_rows[:, i, :], in_=tanh_c[:, i, :])
-
-        def readout_block(block):
-            first = GATE_CHUNKS + block * PASSES
-            for i in range(B_TILES):
-                y = y_pool.tile([P, CHUNK_COLS], F32, tag="y")
-                rows = slice(i * P, (i + 1) * P)
-                for half in range(HALVES):
-                    cols = slice(half * N_TILE, (half + 1) * N_TILE)
-                    acc = psum.tile([P, N_TILE], F32, tag="bank")
-                    for g in range(PASSES):
-                        nc.tensor.matmul_mx(
-                            out=acc[:],
-                            lhsT=ht_codes[:, g, rows].bitcast(FP8X4),
-                            lhsT_scale=ht_scales[:, g, rows],
-                            rhs=codes_of[first + g][:, cols].bitcast(FP8X4),
-                            rhs_scale=scales_of[first + g][:, cols],
-                            start=(g == 0),
-                            stop=(g == PASSES - 1),
-                        )
-                    nc.scalar.activation(out=y[:, cols], in_=acc[:], func=ACT.Sigmoid)
-                nc.sync.dma_start(
-                    out=yt_rows[:, i, block * CHUNK_COLS : (block + 1) * CHUNK_COLS], in_=y[:]
-                )
-
-        def finish(j):
+        def finish_gate_unit(j):
             quantise(j)
-            if j < GATE_CHUNKS:
-                gate_passes(j)
-                if j == GATE_CHUNKS - 1:
-                    gate_epilogue()
-            elif (j - GATE_CHUNKS) % PASSES == PASSES - 1:
-                readout_block((j - GATE_CHUNKS) // PASSES)
+            for i in range(EARLY_TILES):
+                for half in range(HALVES):
+                    gate_pass(j, i, half)
 
-        for j in range(WEIGHT_CHUNKS):
+        for j in range(GATE_CHUNKS):
             regroup(j)
+            if j < B_TILES:
+                tanh_tile(j)
             if j > 0:
-                finish(j - 1)
-        finish(WEIGHT_CHUNKS - 1)
+                finish_gate_unit(j - 1)
+        finish_gate_unit(GATE_CHUNKS - 1)
+
+        hidden_state(0)
+        for i in range(EARLY_TILES, B_TILES):
+            for half in range(HALVES):
+                for j in range(GATE_CHUNKS):
+                    gate_pass(j, i, half)
+        for i in range(1, B_TILES):
+            hidden_state(i)
+            quantise_hidden_state(i - 1)
+        quantise_hidden_state(B_TILES - 1)
+
+        for unit in range(GATE_CHUNKS, UNITS):
+            regroup(unit)
+            if unit > GATE_CHUNKS:
+                quantise(unit - 1)
+                readout_passes(unit - 1)
+        quantise(UNITS - 1)
+        readout_passes(UNITS - 1)

@@ -31,13 +31,8 @@ READOUT_BLOCKS = VOCAB // CHUNK_COLS
 N_BLOCKS = VOCAB // N_TILE
 UNITS = GATE_CHUNKS + N_BLOCKS
 
-BANK_COLS = 256
-GATE_TENSOR_COLS = 512
-READOUT_TENSOR_COLS = 256
-
-SUM_BANKS = 6
-SPARE_BANKS = 2
-EARLY_TILES = SUM_BANKS // HALVES
+GATE_SHARED_VECTOR_COLS = 0
+READOUT_SHARED_VECTOR_COLS = 416
 
 RAW_BUFS = 8
 
@@ -70,30 +65,32 @@ def tile_lstm_peephole_build_pb_kernel(
         keep = ctx.enter_context(tc.tile_pool(name="keep", bufs=1))
         raw_pool = ctx.enter_context(tc.tile_pool(name="raw", bufs=RAW_BUFS))
         grouped_pool = ctx.enter_context(tc.tile_pool(name="grouped", bufs=4))
-        gate_codes_pool = ctx.enter_context(tc.tile_pool(name="gate_codes", bufs=GATE_CHUNKS))
-        codes_pool = ctx.enter_context(tc.tile_pool(name="codes", bufs=4))
-        sig_pool = ctx.enter_context(tc.tile_pool(name="sig", bufs=3))
-        y_pool = ctx.enter_context(tc.tile_pool(name="y", bufs=6))
-        sums = ctx.enter_context(tc.psum_pool(name="sums", bufs=SUM_BANKS))
-        spare = ctx.enter_context(tc.psum_pool(name="spare", bufs=SPARE_BANKS))
+        codes_pool = ctx.enter_context(tc.tile_pool(name="codes", bufs=6))
+        sig_pool = ctx.enter_context(tc.tile_pool(name="sig", bufs=B_TILES * PASSES))
+        y_pool = ctx.enter_context(tc.tile_pool(name="y", bufs=2 * B_TILES))
+        psum = ctx.enter_context(tc.psum_pool(name="psum", bufs=8))
+        ctx.enter_context(tc.manual_schedule())
 
         raws = {}
 
-        def load(j):
-            if j < len(sources):
-                raw = raw_pool.tile([P, CHUNK_ELEMS], BF16, tag="raw")
-                runs = sources[j].shape[1]
-                dst = raw[:].rearrange("p (r m) -> p r m", r=runs)
-                pieces = runs if j == 0 else 1
-                step = runs // pieces
-                for r in range(0, runs, step):
-                    nc.sync.dma_start(out=dst[:, r : r + step, :], in_=sources[j][:, r : r + step, :])
-                raws[j] = raw
+        def load(j, first):
+            raw = raw_pool.tile([P, CHUNK_ELEMS], BF16, tag="raw")
+            runs = sources[j].shape[1]
+            dst = raw[:].rearrange("p (r m) -> p r m", r=runs)
+            step = 1 if first else runs
+            for r in range(0, runs, step):
+                nc.sync.dma_start(out=dst[:, r : r + step, :], in_=sources[j][:, r : r + step, :])
+            raws[j] = raw
 
         loaded = []
 
+        load_order = list(range(len(sources)))
+        load_order[N_ACTS - 1] = N_ACTS
+        load_order[N_ACTS] = N_ACTS - 1
+
         def load_next():
-            load(len(loaded))
+            if len(loaded) < len(sources):
+                load(load_order[len(loaded)], first=(len(loaded) == 0))
             loaded.append(True)
 
         for j in range(RAW_BUFS):
@@ -101,8 +98,6 @@ def tile_lstm_peephole_build_pb_kernel(
 
         ident = const.tile([P, P], F32)
         make_identity(nc, ident[:])
-        ident_bf = const.tile([P, P], BF16)
-        make_identity(nc, ident_bf[:])
 
         warm = const.tile([P, 1], F32)
         nc.vector.memset(warm[:], 0.0)
@@ -112,13 +107,13 @@ def tile_lstm_peephole_build_pb_kernel(
         act_scales = keep.tile([P, N_ACTS, B_TILES * PASSES * P], U8, align_bytes=64)
         tanh_c = keep.tile([P, B_TILES, HIDDEN], F32)
 
-        for a in range(N_ACTS):
+        def transpose_and_quantise(a):
             words = raws[a][:].bitcast(F32)
             grouped = grouped_pool.tile([P, CHUNK_ELEMS], BF16, tag="grouped", align_bytes=64)
             grouped_words = grouped[:].bitcast(F32)
             words_per_tile = HIDDEN // 2
             for i in range(B_TILES):
-                bank = spare.tile([P, PASSES * 2, P], F32, tag="bank")
+                bank = psum.tile([P, PASSES * 2, P], F32, tag="bank")
                 for w in range(PASSES * 2):
                     first = i * words_per_tile + w * P
                     nc.tensor.transpose(bank[:, w, :], words[:, first : first + P], ident[:])
@@ -158,33 +153,17 @@ def tile_lstm_peephole_build_pb_kernel(
         def regroup(unit):
             grouped = grouped_pool.tile([P, CHUNK_ELEMS], BF16, tag="grouped", align_bytes=64)
             dst = grouped[:].rearrange("p (s c r t) -> p s c t r", s=2, r=RUN, t=PACK)
-            tensor_cols = GATE_TENSOR_COLS if unit < GATE_CHUNKS else READOUT_TENSOR_COLS
-            vector_cols = N_TILE - tensor_cols
+            shared = GATE_SHARED_VECTOR_COLS if unit < GATE_CHUNKS else READOUT_SHARED_VECTOR_COLS
+            split = shared // RUN
             for s, (j, col) in enumerate(parts_of(unit)):
                 src = raws[j][:].rearrange("p (t c r) -> p c t r", t=PACK, r=RUN)
                 src = src[:, col // RUN : (col + N_TILE) // RUN, :, :]
                 if s == 0:
                     nc.vector.tensor_copy(out=dst[:, s, :, :, :], in_=src)
-                    continue
-                if vector_cols > 0:
-                    split = vector_cols // RUN
-                    nc.vector.tensor_copy(out=dst[:, s, :split, :, :], in_=src[:, :split, :, :])
-                rows = raws[j][:].rearrange("p (t n) -> p t n", t=PACK)
-                for first in range(vector_cols, N_TILE, BANK_COLS):
-                    bank = spare.tile([P, BANK_COLS, PACK], BF16, tag="bank")
-                    for n in range(0, BANK_COLS, P):
-                        nc.tensor.matmul(
-                            out=bank[:, n : n + P, :].rearrange("p n t -> p t n"),
-                            lhsT=ident_bf[:],
-                            rhs=rows[:, :, col + first + n : col + first + n + P],
-                            start=True,
-                            stop=True,
-                        )
-                    place = (N_TILE + first) * PACK
-                    nc.scalar.copy(
-                        out=grouped[:, place : place + BANK_COLS * PACK],
-                        in_=bank[:].rearrange("p n t -> p (n t)"),
-                    )
+                else:
+                    if split > 0:
+                        nc.vector.tensor_copy(out=dst[:, s, :split, :, :], in_=src[:, :split, :, :])
+                    nc.scalar.copy(out=dst[:, s, split:, :, :], in_=src[:, split:, :, :])
             grouped_of[unit] = grouped
             if unit < GATE_CHUNKS:
                 load_next()
@@ -193,9 +172,8 @@ def tile_lstm_peephole_build_pb_kernel(
                     load_next()
 
         def quantise(unit):
-            pool = gate_codes_pool if unit < GATE_CHUNKS else codes_pool
-            codes = pool.tile([P, 2, N_TILE], U32, tag="codes", align_bytes=64)
-            scales = pool.tile([P, 2, N_TILE], U8, tag="scales", align_bytes=64)
+            codes = codes_pool.tile([P, 2, N_TILE], U32, tag="codes", align_bytes=64)
+            scales = codes_pool.tile([P, 2, N_TILE], U8, tag="scales", align_bytes=64)
             nc.vector.quantize_mx(
                 out=codes[:].rearrange("p s n -> p (s n)").bitcast(FP8X4),
                 scales=scales[:].rearrange("p s n -> p (s n)"),
@@ -206,51 +184,50 @@ def tile_lstm_peephole_build_pb_kernel(
 
         zo = {}
 
-        def gate_pass(j, i, half):
+        def gate_passes(j):
             a, g = divmod(j, PASSES)
-            if j == 0:
-                zo[(i, half)] = sums.tile([P, N_TILE], F32, tag="sum", name="zo")
-            rows = slice((i * PASSES + g) * P, (i * PASSES + g + 1) * P)
-            nc.tensor.matmul_mx(
-                out=zo[(i, half)][:],
-                lhsT=act_codes[:, a, rows].bitcast(FP8X4),
-                lhsT_scale=act_scales[:, a, rows],
-                rhs=codes_of[j][:, half, :].bitcast(FP8X4),
-                rhs_scale=scales_of[j][:, half, :],
-                start=(j == 0),
-                stop=(j == GATE_CHUNKS - 1),
-            )
-
-        ht_grouped = keep.tile([P, B_TILES, PASSES * P * PACK], BF16, align_bytes=64)
-        ht_codes = keep.tile([P, B_TILES, PASSES * P], U32, align_bytes=64)
-        ht_scales = keep.tile([P, B_TILES, PASSES * P], U8, align_bytes=64)
-
-        def hidden_state(i):
-            sig = sig_pool.tile([P, HIDDEN], F32, tag="sig")
             for half in range(HALVES):
-                nc.scalar.activation(
-                    out=sig[:, half * N_TILE : (half + 1) * N_TILE],
-                    in_=zo[(i, half)][:],
-                    func=ACT.Sigmoid,
-                )
-            nc.vector.tensor_mul(out=tanh_c[:, i, :], in0=sig[:], in1=tanh_c[:, i, :])
-            nc.sync.dma_start(out=ht_rows[:, i, :], in_=tanh_c[:, i, :])
+                for i in range(B_TILES):
+                    if j == 0:
+                        zo[(i, half)] = psum.tile([P, N_TILE], F32, tag="bank", name="zo")
+                    rows = slice((i * PASSES + g) * P, (i * PASSES + g + 1) * P)
+                    nc.tensor.matmul_mx(
+                        out=zo[(i, half)][:],
+                        lhsT=act_codes[:, a, rows].bitcast(FP8X4),
+                        lhsT_scale=act_scales[:, a, rows],
+                        rhs=codes_of[j][:, half, :].bitcast(FP8X4),
+                        rhs_scale=scales_of[j][:, half, :],
+                        start=(j == 0),
+                        stop=(j == GATE_CHUNKS - 1),
+                    )
 
-        def quantise_hidden_state(i):
-            for g in range(PASSES):
-                bank = spare.tile([P, PACK, P], F32, tag="bank")
+        ht_grouped = keep.tile([P, PASSES, B_TILES * P * PACK], BF16, align_bytes=64)
+        ht_codes = keep.tile([P, PASSES, B_TILES * P], U32, align_bytes=64)
+        ht_scales = keep.tile([P, PASSES, B_TILES * P], U8, align_bytes=64)
+
+        def hidden_state(g, i):
+            sig = sig_pool.tile([P, N_TILE], F32, tag="sig")
+            nc.scalar.activation(out=sig[:], in_=zo[(i, g)][:], func=ACT.Sigmoid)
+            ht = tanh_c[:, i, g * K_PASS : (g + 1) * K_PASS]
+            nc.vector.tensor_mul(out=ht, in0=sig[:], in1=ht)
+
+        def transpose_hidden_state(g):
+            for i in range(B_TILES):
+                bank = psum.tile([P, PACK, P], F32, tag="bank")
                 for t in range(PACK):
                     first = g * K_PASS + t * P
                     nc.tensor.transpose(bank[:, t, :], tanh_c[:, i, first : first + P], ident[:])
-                dst = ht_grouped[:, i, g * K_PASS : (g + 1) * K_PASS]
+                dst = ht_grouped[:, g, i * K_PASS : (i + 1) * K_PASS]
                 nc.scalar.copy(
                     out=dst.rearrange("p (b t) -> p b t", t=PACK),
                     in_=bank[:].rearrange("p t b -> p b t"),
                 )
+
+        def quantise_hidden_state(g):
             nc.vector.quantize_mx(
-                out=ht_codes[:, i, :].bitcast(FP8X4),
-                scales=ht_scales[:, i, :],
-                in_=ht_grouped[:, i, :],
+                out=ht_codes[:, g, :].bitcast(FP8X4),
+                scales=ht_scales[:, g, :],
+                in_=ht_grouped[:, g, :],
             )
 
         y_of = {}
@@ -260,13 +237,13 @@ def tile_lstm_peephole_build_pb_kernel(
             for i in range(B_TILES):
                 if half == 0:
                     y_of[i] = y_pool.tile([P, CHUNK_COLS], F32, tag="y", name="y")
-                acc = sums.tile([P, N_TILE], F32, tag="sum")
+                rows = slice(i * P, (i + 1) * P)
+                acc = psum.tile([P, N_TILE], F32, tag="bank")
                 for g in range(PASSES):
-                    rows = slice(g * P, (g + 1) * P)
                     nc.tensor.matmul_mx(
                         out=acc[:],
-                        lhsT=ht_codes[:, i, rows].bitcast(FP8X4),
-                        lhsT_scale=ht_scales[:, i, rows],
+                        lhsT=ht_codes[:, g, rows].bitcast(FP8X4),
+                        lhsT_scale=ht_scales[:, g, rows],
                         rhs=codes_of[unit][:, g, :].bitcast(FP8X4),
                         rhs_scale=scales_of[unit][:, g, :],
                         start=(g == 0),
@@ -275,40 +252,46 @@ def tile_lstm_peephole_build_pb_kernel(
                 nc.scalar.activation(
                     out=y_of[i][:, half * N_TILE : (half + 1) * N_TILE], in_=acc[:], func=ACT.Sigmoid
                 )
-                if half == HALVES - 1:
+                first = block * CHUNK_COLS
+                if block == READOUT_BLOCKS - 1:
+                    cols = slice(half * N_TILE, (half + 1) * N_TILE)
                     nc.sync.dma_start(
-                        out=yt_rows[:, i, block * CHUNK_COLS : (block + 1) * CHUNK_COLS],
-                        in_=y_of[i][:],
+                        out=yt_rows[:, i, first + half * N_TILE : first + (half + 1) * N_TILE],
+                        in_=y_of[i][:, cols],
+                    )
+                elif half == HALVES - 1:
+                    nc.sync.dma_start(
+                        out=yt_rows[:, i, first : first + CHUNK_COLS], in_=y_of[i][:]
                     )
 
-        def finish_gate_unit(j):
-            quantise(j)
-            for i in range(EARLY_TILES):
-                for half in range(HALVES):
-                    gate_pass(j, i, half)
+        def prepare(unit):
+            if unit < UNITS:
+                regroup(unit)
+            if unit <= UNITS:
+                quantise(unit - 1)
 
-        for j in range(GATE_CHUNKS):
-            regroup(j)
-            if j < B_TILES:
-                tanh_tile(j)
-            if j > 0:
-                finish_gate_unit(j - 1)
-        finish_gate_unit(GATE_CHUNKS - 1)
+        transpose_and_quantise(0)
+        transpose_and_quantise(1)
+        regroup(0)
+        transpose_and_quantise(2)
+        for j in range(1, GATE_CHUNKS + 1):
+            prepare(j)
+            gate_passes(j - 1)
+            if j <= B_TILES:
+                tanh_tile(j - 1)
 
-        hidden_state(0)
-        for i in range(EARLY_TILES, B_TILES):
-            for half in range(HALVES):
-                for j in range(GATE_CHUNKS):
-                    gate_pass(j, i, half)
-        for i in range(1, B_TILES):
-            hidden_state(i)
-            quantise_hidden_state(i - 1)
-        quantise_hidden_state(B_TILES - 1)
+        prepare(GATE_CHUNKS + 1)
+        for g in range(PASSES):
+            for i in range(B_TILES):
+                hidden_state(g, i)
+        transpose_hidden_state(0)
+        prepare(GATE_CHUNKS + 2)
+        quantise_hidden_state(0)
+        transpose_hidden_state(1)
+        quantise_hidden_state(1)
+        for i in range(B_TILES):
+            nc.sync.dma_start(out=ht_rows[:, i, :], in_=tanh_c[:, i, :])
 
         for unit in range(GATE_CHUNKS, UNITS):
-            regroup(unit)
-            if unit > GATE_CHUNKS:
-                quantise(unit - 1)
-                readout_passes(unit - 1)
-        quantise(UNITS - 1)
-        readout_passes(UNITS - 1)
+            readout_passes(unit)
+            prepare(unit + 3)

@@ -26,7 +26,9 @@ RUN = 4
 
 N_ACTS = 3
 GATE_CHUNKS = N_ACTS * PASSES
-READOUT_BLOCKS = VOCAB // CHUNK_COLS
+READOUT_COLS = 2048
+READOUT_BLOCKS = VOCAB // READOUT_COLS
+READOUT_ELEMS = PACK * READOUT_COLS
 
 N_BLOCKS = VOCAB // N_TILE
 UNITS = GATE_CHUNKS + N_BLOCKS
@@ -34,7 +36,7 @@ UNITS = GATE_CHUNKS + N_BLOCKS
 GATE_SHARED_VECTOR_COLS = 0
 READOUT_SHARED_VECTOR_COLS = 416
 
-RAW_BUFS = 8
+RAW_BUFS = 5
 
 FLOPS = 2 * BATCH * HIDDEN * (N_ACTS * HIDDEN + VOCAB)
 
@@ -56,7 +58,7 @@ def tile_lstm_peephole_build_pb_kernel(
     for block in range(READOUT_BLOCKS):
         for g in range(PASSES):
             rows = w_op[
-                g * K_PASS : (g + 1) * K_PASS, block * CHUNK_COLS : (block + 1) * CHUNK_COLS
+                g * K_PASS : (g + 1) * K_PASS, block * READOUT_COLS : (block + 1) * READOUT_COLS
             ]
             sources.append(rows.rearrange("(t p) n -> p t n", p=P))
 
@@ -66,7 +68,7 @@ def tile_lstm_peephole_build_pb_kernel(
         raw_pool = ctx.enter_context(tc.tile_pool(name="raw", bufs=RAW_BUFS))
         grouped_pool = ctx.enter_context(tc.tile_pool(name="grouped", bufs=4))
         codes_pool = ctx.enter_context(tc.tile_pool(name="codes", bufs=6))
-        sig_pool = ctx.enter_context(tc.tile_pool(name="sig", bufs=B_TILES * PASSES))
+        wide_pool = ctx.enter_context(tc.tile_pool(name="wide", bufs=READOUT_BLOCKS * PASSES))
         y_pool = ctx.enter_context(tc.tile_pool(name="y", bufs=2 * B_TILES))
         psum = ctx.enter_context(tc.psum_pool(name="psum", bufs=8))
         ctx.enter_context(tc.manual_schedule())
@@ -74,7 +76,10 @@ def tile_lstm_peephole_build_pb_kernel(
         raws = {}
 
         def load(j, first):
-            raw = raw_pool.tile([P, CHUNK_ELEMS], BF16, tag="raw")
+            if j < N_ACTS + GATE_CHUNKS:
+                raw = raw_pool.tile([P, CHUNK_ELEMS], BF16, tag="raw")
+            else:
+                raw = wide_pool.tile([P, READOUT_ELEMS], BF16, tag="wide", name="raw")
             runs = sources[j].shape[1]
             dst = raw[:].rearrange("p (r m) -> p r m", r=runs)
             step = 1 if first else runs
@@ -89,8 +94,7 @@ def tile_lstm_peephole_build_pb_kernel(
         load_order[N_ACTS] = N_ACTS - 1
 
         def load_next():
-            if len(loaded) < len(sources):
-                load(load_order[len(loaded)], first=(len(loaded) == 0))
+            load(load_order[len(loaded)], first=(len(loaded) == 0))
             loaded.append(True)
 
         for j in range(RAW_BUFS):
@@ -137,14 +141,15 @@ def tile_lstm_peephole_build_pb_kernel(
                 func=ACT.Tanh,
             )
             if i == B_TILES - 1:
-                load_next()
+                for j in range(1 + READOUT_BLOCKS * PASSES):
+                    load_next()
 
         def parts_of(unit):
             if unit < GATE_CHUNKS:
                 return [(N_ACTS + unit, 0), (N_ACTS + unit, N_TILE)]
-            block, half = divmod(unit - GATE_CHUNKS, HALVES)
+            block, quarter = divmod(unit - GATE_CHUNKS, READOUT_COLS // N_TILE)
             first = N_ACTS + GATE_CHUNKS + block * PASSES
-            return [(first + g, half * N_TILE) for g in range(PASSES)]
+            return [(first + g, quarter * N_TILE) for g in range(PASSES)]
 
         grouped_of = {}
         codes_of = {}
@@ -165,11 +170,8 @@ def tile_lstm_peephole_build_pb_kernel(
                         nc.vector.tensor_copy(out=dst[:, s, :split, :, :], in_=src[:, :split, :, :])
                     nc.scalar.copy(out=dst[:, s, split:, :, :], in_=src[:, split:, :, :])
             grouped_of[unit] = grouped
-            if unit < GATE_CHUNKS:
+            if unit == 0:
                 load_next()
-            elif (unit - GATE_CHUNKS) % HALVES == HALVES - 1:
-                for g in range(PASSES):
-                    load_next()
 
         def quantise(unit):
             codes = codes_pool.tile([P, 2, N_TILE], U32, tag="codes", align_bytes=64)
@@ -201,23 +203,27 @@ def tile_lstm_peephole_build_pb_kernel(
                         stop=(j == GATE_CHUNKS - 1),
                     )
 
-        ht_grouped = keep.tile([P, PASSES, B_TILES * P * PACK], BF16, align_bytes=64)
         ht_codes = keep.tile([P, PASSES, B_TILES * P], U32, align_bytes=64)
         ht_scales = keep.tile([P, PASSES, B_TILES * P], U8, align_bytes=64)
 
         def hidden_state(g, i):
-            sig = sig_pool.tile([P, N_TILE], F32, tag="sig")
+            sig = y_pool.tile([P, N_TILE], F32, tag="y", name="sig")
             nc.scalar.activation(out=sig[:], in_=zo[(i, g)][:], func=ACT.Sigmoid)
             ht = tanh_c[:, i, g * K_PASS : (g + 1) * K_PASS]
             nc.vector.tensor_mul(out=ht, in0=sig[:], in1=ht)
 
+        ht_grouped = []
+
         def transpose_hidden_state(g):
+            if g == 0:
+                tile = grouped_pool.tile([P, CHUNK_ELEMS], BF16, tag="grouped", align_bytes=64)
+                ht_grouped.append(tile[:].rearrange("p (g m) -> p g m", g=PASSES))
             for i in range(B_TILES):
                 bank = psum.tile([P, PACK, P], F32, tag="bank")
                 for t in range(PACK):
                     first = g * K_PASS + t * P
                     nc.tensor.transpose(bank[:, t, :], tanh_c[:, i, first : first + P], ident[:])
-                dst = ht_grouped[:, g, i * K_PASS : (i + 1) * K_PASS]
+                dst = ht_grouped[0][:, g, i * K_PASS : (i + 1) * K_PASS]
                 nc.scalar.copy(
                     out=dst.rearrange("p (b t) -> p b t", t=PACK),
                     in_=bank[:].rearrange("p t b -> p b t"),
@@ -227,7 +233,7 @@ def tile_lstm_peephole_build_pb_kernel(
             nc.vector.quantize_mx(
                 out=ht_codes[:, g, :].bitcast(FP8X4),
                 scales=ht_scales[:, g, :],
-                in_=ht_grouped[:, g, :],
+                in_=ht_grouped[0][:, g, :],
             )
 
         y_of = {}
@@ -253,7 +259,7 @@ def tile_lstm_peephole_build_pb_kernel(
                     out=y_of[i][:, half * N_TILE : (half + 1) * N_TILE], in_=acc[:], func=ACT.Sigmoid
                 )
                 first = block * CHUNK_COLS
-                if block == READOUT_BLOCKS - 1:
+                if block == VOCAB // CHUNK_COLS - 1:
                     cols = slice(half * N_TILE, (half + 1) * N_TILE)
                     nc.sync.dma_start(
                         out=yt_rows[:, i, first + half * N_TILE : first + (half + 1) * N_TILE],
@@ -277,8 +283,9 @@ def tile_lstm_peephole_build_pb_kernel(
         for j in range(1, GATE_CHUNKS + 1):
             prepare(j)
             gate_passes(j - 1)
-            if j <= B_TILES:
-                tanh_tile(j - 1)
+            if j <= B_TILES // 2:
+                tanh_tile(2 * j - 2)
+                tanh_tile(2 * j - 1)
 
         prepare(GATE_CHUNKS + 1)
         for g in range(PASSES):

@@ -26,9 +26,8 @@ RUN = 4
 
 N_ACTS = 3
 GATE_CHUNKS = N_ACTS * PASSES
-READOUT_COLS = 2048
-READOUT_BLOCKS = VOCAB // READOUT_COLS
-READOUT_ELEMS = PACK * READOUT_COLS
+READOUT_COLS = ((0, 1024), (1024, 4096))
+READOUT_CHUNKS = PASSES * len(READOUT_COLS)
 
 N_BLOCKS = VOCAB // N_TILE
 UNITS = GATE_CHUNKS + N_BLOCKS
@@ -36,7 +35,7 @@ UNITS = GATE_CHUNKS + N_BLOCKS
 GATE_SHARED_VECTOR_COLS = 0
 READOUT_SHARED_VECTOR_COLS = 416
 
-RAW_BUFS = 5
+RAW_BUFS = 4
 
 FLOPS = 2 * BATCH * HIDDEN * (N_ACTS * HIDDEN + VOCAB)
 
@@ -49,17 +48,15 @@ def tile_lstm_peephole_build_pb_kernel(
     ht_rows = out_1.rearrange("(p i) n -> p i n", i=B_TILES)
 
     sources = []
-    for act in (input_data, previous_hidden_state, c_t):
+    for act in (c_t, input_data, previous_hidden_state):
         sources.append(act.rearrange("(p i) k -> p i k", i=B_TILES))
-    for weight in (w_ip_o, w_output, w_output_c):
+    for weight in (w_output_c, w_ip_o, w_output):
         for g in range(PASSES):
             rows = weight[g * K_PASS : (g + 1) * K_PASS, :]
             sources.append(rows.rearrange("(u q e) n -> q u (e n)", u=2, e=2))
-    for block in range(READOUT_BLOCKS):
+    for low, high in READOUT_COLS:
         for g in range(PASSES):
-            rows = w_op[
-                g * K_PASS : (g + 1) * K_PASS, block * READOUT_COLS : (block + 1) * READOUT_COLS
-            ]
+            rows = w_op[g * K_PASS : (g + 1) * K_PASS, low:high]
             sources.append(rows.rearrange("(t p) n -> p t n", p=P))
 
     with ExitStack() as ctx:
@@ -68,18 +65,21 @@ def tile_lstm_peephole_build_pb_kernel(
         raw_pool = ctx.enter_context(tc.tile_pool(name="raw", bufs=RAW_BUFS))
         grouped_pool = ctx.enter_context(tc.tile_pool(name="grouped", bufs=4))
         codes_pool = ctx.enter_context(tc.tile_pool(name="codes", bufs=6))
-        wide_pool = ctx.enter_context(tc.tile_pool(name="wide", bufs=READOUT_BLOCKS * PASSES))
-        y_pool = ctx.enter_context(tc.tile_pool(name="y", bufs=2 * B_TILES))
+        wide_pool = ctx.enter_context(tc.tile_pool(name="wide", bufs=1))
+        y_pool = ctx.enter_context(tc.tile_pool(name="y", bufs=4 * B_TILES))
         psum = ctx.enter_context(tc.psum_pool(name="psum", bufs=8))
         ctx.enter_context(tc.manual_schedule())
 
         raws = {}
 
         def load(j, first):
-            if j < N_ACTS + GATE_CHUNKS:
+            if j == 0:
+                raw = keep.tile([P, CHUNK_ELEMS], BF16, tag="c", name="raw")
+            elif j < N_ACTS + GATE_CHUNKS:
                 raw = raw_pool.tile([P, CHUNK_ELEMS], BF16, tag="raw")
             else:
-                raw = wide_pool.tile([P, READOUT_ELEMS], BF16, tag="wide", name="raw")
+                cols = sources[j].shape[2]
+                raw = wide_pool.tile([P, PACK * cols], BF16, tag="wide" + str(j), name="raw")
             runs = sources[j].shape[1]
             dst = raw[:].rearrange("p (r m) -> p r m", r=runs)
             step = 1 if first else runs
@@ -97,7 +97,7 @@ def tile_lstm_peephole_build_pb_kernel(
             load(load_order[len(loaded)], first=(len(loaded) == 0))
             loaded.append(True)
 
-        for j in range(RAW_BUFS):
+        for j in range(RAW_BUFS + 1):
             load_next()
 
         ident = const.tile([P, P], F32)
@@ -124,54 +124,66 @@ def tile_lstm_peephole_build_pb_kernel(
                 dst = grouped_words[:, i * words_per_tile : (i + 1) * words_per_tile]
                 dst = dst.rearrange("p (g b u) -> p g b u", g=PASSES, u=2)
                 src = bank[:].rearrange("p (g u) b -> p g b u", u=2)
-                if i % 2 == 0:
+                if a > 0 and i % 2 == 0:
                     nc.scalar.copy(out=dst, in_=src)
                 else:
                     nc.vector.tensor_copy(out=dst, in_=src)
             nc.vector.quantize_mx(
                 out=act_codes[:, a, :].bitcast(FP8X4), scales=act_scales[:, a, :], in_=grouped[:]
             )
-            if a < N_ACTS - 1:
+            if a > 0:
                 load_next()
 
         def tanh_tile(i):
             nc.scalar.activation(
                 out=tanh_c[:, i, :],
-                in_=raws[N_ACTS - 1][:, i * HIDDEN : (i + 1) * HIDDEN],
+                in_=raws[0][:, i * HIDDEN : (i + 1) * HIDDEN],
                 func=ACT.Tanh,
             )
-            if i == B_TILES - 1:
-                for j in range(1 + READOUT_BLOCKS * PASSES):
-                    load_next()
+
+        def readout_part(n, g):
+            for block, (low, high) in enumerate(READOUT_COLS):
+                if low <= n * N_TILE < high:
+                    return N_ACTS + GATE_CHUNKS + block * PASSES + g, n * N_TILE - low
 
         def parts_of(unit):
             if unit < GATE_CHUNKS:
                 return [(N_ACTS + unit, 0), (N_ACTS + unit, N_TILE)]
-            block, quarter = divmod(unit - GATE_CHUNKS, READOUT_COLS // N_TILE)
-            first = N_ACTS + GATE_CHUNKS + block * PASSES
-            return [(first + g, quarter * N_TILE) for g in range(PASSES)]
+            return [readout_part(unit - GATE_CHUNKS, g) for g in range(PASSES)]
 
         grouped_of = {}
         codes_of = {}
         scales_of = {}
 
-        def regroup(unit):
-            grouped = grouped_pool.tile([P, CHUNK_ELEMS], BF16, tag="grouped", align_bytes=64)
-            dst = grouped[:].rearrange("p (s c r t) -> p s c t r", s=2, r=RUN, t=PACK)
+        def regroup_views(unit, s):
+            j, col = parts_of(unit)[s]
+            dst = grouped_of[unit][:].rearrange("p (s c r t) -> p s c t r", s=2, r=RUN, t=PACK)
+            src = raws[j][:].rearrange("p (t c r) -> p c t r", t=PACK, r=RUN)
+            return dst[:, s, :, :, :], src[:, col // RUN : (col + N_TILE) // RUN, :, :]
+
+        def regroup_first(unit):
+            grouped_of[unit] = grouped_pool.tile(
+                [P, CHUNK_ELEMS], BF16, tag="grouped", name="grouped", align_bytes=64
+            )
+            dst, src = regroup_views(unit, 0)
+            nc.vector.tensor_copy(out=dst, in_=src)
+
+        def regroup_second(unit):
             shared = GATE_SHARED_VECTOR_COLS if unit < GATE_CHUNKS else READOUT_SHARED_VECTOR_COLS
             split = shared // RUN
-            for s, (j, col) in enumerate(parts_of(unit)):
-                src = raws[j][:].rearrange("p (t c r) -> p c t r", t=PACK, r=RUN)
-                src = src[:, col // RUN : (col + N_TILE) // RUN, :, :]
-                if s == 0:
-                    nc.vector.tensor_copy(out=dst[:, s, :, :, :], in_=src)
-                else:
-                    if split > 0:
-                        nc.vector.tensor_copy(out=dst[:, s, :split, :, :], in_=src[:, :split, :, :])
-                    nc.scalar.copy(out=dst[:, s, split:, :, :], in_=src[:, split:, :, :])
-            grouped_of[unit] = grouped
-            if unit == 0:
+            dst, src = regroup_views(unit, 1)
+            nc.scalar.copy(out=dst[:, split:, :, :], in_=src[:, split:, :, :])
+            if split > 0:
+                nc.vector.tensor_copy(out=dst[:, :split, :, :], in_=src[:, :split, :, :])
+            if unit < 2:
                 load_next()
+            if unit == 1:
+                for j in range(READOUT_CHUNKS):
+                    load_next()
+
+        def regroup(unit):
+            regroup_first(unit)
+            regroup_second(unit)
 
         def quantise(unit):
             codes = codes_pool.tile([P, 2, N_TILE], U32, tag="codes", align_bytes=64)
@@ -181,8 +193,9 @@ def tile_lstm_peephole_build_pb_kernel(
                 scales=scales[:].rearrange("p s n -> p (s n)"),
                 in_=grouped_of[unit][:],
             )
-            codes_of[unit] = codes
-            scales_of[unit] = scales
+            for s, part in enumerate(parts_of(unit)):
+                codes_of[part] = codes[:, s, :].bitcast(FP8X4)
+                scales_of[part] = scales[:, s, :]
 
         zo = {}
 
@@ -197,8 +210,8 @@ def tile_lstm_peephole_build_pb_kernel(
                         out=zo[(i, half)][:],
                         lhsT=act_codes[:, a, rows].bitcast(FP8X4),
                         lhsT_scale=act_scales[:, a, rows],
-                        rhs=codes_of[j][:, half, :].bitcast(FP8X4),
-                        rhs_scale=scales_of[j][:, half, :],
+                        rhs=codes_of[(N_ACTS + j, half * N_TILE)],
+                        rhs_scale=scales_of[(N_ACTS + j, half * N_TILE)],
                         start=(j == 0),
                         stop=(j == GATE_CHUNKS - 1),
                     )
@@ -236,13 +249,9 @@ def tile_lstm_peephole_build_pb_kernel(
                 in_=ht_grouped[0][:, g, :],
             )
 
-        y_of = {}
-
-        def readout_passes(unit):
-            block, half = divmod(unit - GATE_CHUNKS, HALVES)
+        def readout_passes(n):
             for i in range(B_TILES):
-                if half == 0:
-                    y_of[i] = y_pool.tile([P, CHUNK_COLS], F32, tag="y", name="y")
+                y = y_pool.tile([P, N_TILE], F32, tag="y", name="y")
                 rows = slice(i * P, (i + 1) * P)
                 acc = psum.tile([P, N_TILE], F32, tag="bank")
                 for g in range(PASSES):
@@ -250,55 +259,49 @@ def tile_lstm_peephole_build_pb_kernel(
                         out=acc[:],
                         lhsT=ht_codes[:, g, rows].bitcast(FP8X4),
                         lhsT_scale=ht_scales[:, g, rows],
-                        rhs=codes_of[unit][:, g, :].bitcast(FP8X4),
-                        rhs_scale=scales_of[unit][:, g, :],
+                        rhs=codes_of[readout_part(n, g)],
+                        rhs_scale=scales_of[readout_part(n, g)],
                         start=(g == 0),
                         stop=(g == PASSES - 1),
                     )
-                nc.scalar.activation(
-                    out=y_of[i][:, half * N_TILE : (half + 1) * N_TILE], in_=acc[:], func=ACT.Sigmoid
-                )
-                first = block * CHUNK_COLS
-                if block == VOCAB // CHUNK_COLS - 1:
-                    cols = slice(half * N_TILE, (half + 1) * N_TILE)
-                    nc.sync.dma_start(
-                        out=yt_rows[:, i, first + half * N_TILE : first + (half + 1) * N_TILE],
-                        in_=y_of[i][:, cols],
-                    )
-                elif half == HALVES - 1:
-                    nc.sync.dma_start(
-                        out=yt_rows[:, i, first : first + CHUNK_COLS], in_=y_of[i][:]
-                    )
-
-        def prepare(unit):
-            if unit < UNITS:
-                regroup(unit)
-            if unit <= UNITS:
-                quantise(unit - 1)
+                nc.scalar.activation(out=y[:], in_=acc[:], func=ACT.Sigmoid)
+                nc.sync.dma_start(out=yt_rows[:, i, n * N_TILE : (n + 1) * N_TILE], in_=y[:])
 
         transpose_and_quantise(0)
+        for i in range(B_TILES):
+            tanh_tile(i)
         transpose_and_quantise(1)
         regroup(0)
         transpose_and_quantise(2)
-        for j in range(1, GATE_CHUNKS + 1):
-            prepare(j)
+        for j in range(1, GATE_CHUNKS):
+            regroup(j)
+            quantise(j - 1)
             gate_passes(j - 1)
-            if j <= B_TILES // 2:
-                tanh_tile(2 * j - 2)
-                tanh_tile(2 * j - 1)
+        quantise(GATE_CHUNKS - 1)
+        gate_passes(GATE_CHUNKS - 1)
 
-        prepare(GATE_CHUNKS + 1)
-        for g in range(PASSES):
-            for i in range(B_TILES):
-                hidden_state(g, i)
+        first = GATE_CHUNKS
+        regroup(first)
+        for i in range(B_TILES):
+            hidden_state(0, i)
+        quantise(first)
+        for i in range(B_TILES):
+            hidden_state(1, i)
+        regroup(first + 1)
         transpose_hidden_state(0)
-        prepare(GATE_CHUNKS + 2)
-        quantise_hidden_state(0)
         transpose_hidden_state(1)
+        regroup_first(first + 2)
+        quantise(first + 1)
+        quantise_hidden_state(0)
         quantise_hidden_state(1)
         for i in range(B_TILES):
             nc.sync.dma_start(out=ht_rows[:, i, :], in_=tanh_c[:, i, :])
-
-        for unit in range(GATE_CHUNKS, UNITS):
-            readout_passes(unit)
-            prepare(unit + 3)
+        regroup_second(first + 2)
+        for n in range(N_BLOCKS):
+            readout_passes(n)
+            if n + 3 < N_BLOCKS:
+                regroup_first(first + n + 3)
+            if n + 2 < N_BLOCKS:
+                quantise(first + n + 2)
+            if n + 3 < N_BLOCKS:
+                regroup_second(first + n + 3)

@@ -32,7 +32,7 @@ READOUT_CHUNKS = PASSES * len(READOUT_COLS)
 N_BLOCKS = VOCAB // N_TILE
 UNITS = GATE_CHUNKS + N_BLOCKS
 
-GATE_SHARED_VECTOR_COLS = 0
+GATE_SHARED_VECTOR_COLS = 64
 READOUT_SHARED_VECTOR_COLS = 416
 
 RAW_BUFS = 4
@@ -67,8 +67,11 @@ def tile_lstm_peephole_build_pb_kernel(
         codes_pool = ctx.enter_context(tc.tile_pool(name="codes", bufs=6))
         wide_pool = ctx.enter_context(tc.tile_pool(name="wide", bufs=1))
         y_pool = ctx.enter_context(tc.tile_pool(name="y", bufs=4 * B_TILES))
-        psum = ctx.enter_context(tc.psum_pool(name="psum", bufs=8))
+        psum = ctx.enter_context(tc.psum_pool(name="psum", bufs=1))
         ctx.enter_context(tc.manual_schedule())
+
+        def bank_tile(b, shape, name):
+            return psum.tile(shape, F32, tag="bank" + str(b), name=name)
 
         raws = {}
 
@@ -90,8 +93,7 @@ def tile_lstm_peephole_build_pb_kernel(
         loaded = []
 
         load_order = list(range(len(sources)))
-        load_order[N_ACTS - 1] = N_ACTS
-        load_order[N_ACTS] = N_ACTS - 1
+        load_order[1 : N_ACTS + 1] = [N_ACTS, 1, 2]
 
         def load_next():
             load(load_order[len(loaded)], first=(len(loaded) == 0))
@@ -111,28 +113,35 @@ def tile_lstm_peephole_build_pb_kernel(
         act_scales = keep.tile([P, N_ACTS, B_TILES * PASSES * P], U8, align_bytes=64)
         tanh_c = keep.tile([P, B_TILES, HIDDEN], F32)
 
-        def transpose_and_quantise(a):
+        grouped_act = {}
+
+        def transpose(a):
             words = raws[a][:].bitcast(F32)
             grouped = grouped_pool.tile([P, CHUNK_ELEMS], BF16, tag="grouped", align_bytes=64)
             grouped_words = grouped[:].bitcast(F32)
             words_per_tile = HIDDEN // 2
             for i in range(B_TILES):
-                bank = psum.tile([P, PASSES * 2, P], F32, tag="bank")
+                bank = bank_tile(i + (B_TILES if a > 0 else 0), [P, PASSES * 2, P], "bank")
                 for w in range(PASSES * 2):
                     first = i * words_per_tile + w * P
                     nc.tensor.transpose(bank[:, w, :], words[:, first : first + P], ident[:])
                 dst = grouped_words[:, i * words_per_tile : (i + 1) * words_per_tile]
                 dst = dst.rearrange("p (g b u) -> p g b u", g=PASSES, u=2)
                 src = bank[:].rearrange("p (g u) b -> p g b u", u=2)
-                if a > 0 and i % 2 == 0:
+                if a > 0:
                     nc.scalar.copy(out=dst, in_=src)
                 else:
                     nc.vector.tensor_copy(out=dst, in_=src)
-            nc.vector.quantize_mx(
-                out=act_codes[:, a, :].bitcast(FP8X4), scales=act_scales[:, a, :], in_=grouped[:]
-            )
+            grouped_act[a] = grouped
             if a > 0:
                 load_next()
+
+        def quantise_act(a):
+            nc.vector.quantize_mx(
+                out=act_codes[:, a, :].bitcast(FP8X4),
+                scales=act_scales[:, a, :],
+                in_=grouped_act[a][:],
+            )
 
         def tanh_tile(i):
             nc.scalar.activation(
@@ -168,8 +177,13 @@ def tile_lstm_peephole_build_pb_kernel(
             dst, src = regroup_views(unit, 0)
             nc.vector.tensor_copy(out=dst, in_=src)
 
+        def shared_cols(unit):
+            if unit == GATE_CHUNKS:
+                return 0
+            return GATE_SHARED_VECTOR_COLS if unit < GATE_CHUNKS else READOUT_SHARED_VECTOR_COLS
+
         def regroup_second(unit):
-            shared = GATE_SHARED_VECTOR_COLS if unit < GATE_CHUNKS else READOUT_SHARED_VECTOR_COLS
+            shared = shared_cols(unit)
             split = shared // RUN
             dst, src = regroup_views(unit, 1)
             nc.scalar.copy(out=dst[:, split:, :, :], in_=src[:, split:, :, :])
@@ -199,12 +213,12 @@ def tile_lstm_peephole_build_pb_kernel(
 
         zo = {}
 
-        def gate_passes(j):
+        def gate_passes(j, halves=range(HALVES)):
             a, g = divmod(j, PASSES)
-            for half in range(HALVES):
+            for half in halves:
                 for i in range(B_TILES):
                     if j == 0:
-                        zo[(i, half)] = psum.tile([P, N_TILE], F32, tag="bank", name="zo")
+                        zo[(i, half)] = bank_tile(i + B_TILES * half, [P, N_TILE], "zo")
                     rows = slice((i * PASSES + g) * P, (i * PASSES + g + 1) * P)
                     nc.tensor.matmul_mx(
                         out=zo[(i, half)][:],
@@ -232,7 +246,7 @@ def tile_lstm_peephole_build_pb_kernel(
                 tile = grouped_pool.tile([P, CHUNK_ELEMS], BF16, tag="grouped", align_bytes=64)
                 ht_grouped.append(tile[:].rearrange("p (g m) -> p g m", g=PASSES))
             for i in range(B_TILES):
-                bank = psum.tile([P, PACK, P], F32, tag="bank")
+                bank = bank_tile(i + B_TILES * g, [P, PACK, P], "bank")
                 for t in range(PACK):
                     first = g * K_PASS + t * P
                     nc.tensor.transpose(bank[:, t, :], tanh_c[:, i, first : first + P], ident[:])
@@ -253,7 +267,7 @@ def tile_lstm_peephole_build_pb_kernel(
             for i in range(B_TILES):
                 y = y_pool.tile([P, N_TILE], F32, tag="y", name="y")
                 rows = slice(i * P, (i + 1) * P)
-                acc = psum.tile([P, N_TILE], F32, tag="bank")
+                acc = bank_tile(i + B_TILES * (n % HALVES), [P, N_TILE], "acc")
                 for g in range(PASSES):
                     nc.tensor.matmul_mx(
                         out=acc[:],
@@ -267,13 +281,21 @@ def tile_lstm_peephole_build_pb_kernel(
                 nc.scalar.activation(out=y[:], in_=acc[:], func=ACT.Sigmoid)
                 nc.sync.dma_start(out=yt_rows[:, i, n * N_TILE : (n + 1) * N_TILE], in_=y[:])
 
-        transpose_and_quantise(0)
+        transpose(0)
         for i in range(B_TILES):
             tanh_tile(i)
-        transpose_and_quantise(1)
+        quantise_act(0)
         regroup(0)
-        transpose_and_quantise(2)
-        for j in range(1, GATE_CHUNKS):
+        transpose(1)
+        quantise(0)
+        transpose(2)
+        quantise_act(1)
+        gate_passes(0, [0])
+        regroup_first(1)
+        quantise_act(2)
+        regroup_second(1)
+        gate_passes(0, [1])
+        for j in range(2, GATE_CHUNKS):
             regroup(j)
             quantise(j - 1)
             gate_passes(j - 1)
@@ -291,11 +313,11 @@ def tile_lstm_peephole_build_pb_kernel(
         transpose_hidden_state(0)
         transpose_hidden_state(1)
         regroup_first(first + 2)
-        quantise(first + 1)
         quantise_hidden_state(0)
         quantise_hidden_state(1)
         for i in range(B_TILES):
             nc.sync.dma_start(out=ht_rows[:, i, :], in_=tanh_c[:, i, :])
+        quantise(first + 1)
         regroup_second(first + 2)
         for n in range(N_BLOCKS):
             readout_passes(n)

@@ -66,7 +66,7 @@ def tile_lstm_peephole_build_pb_kernel(
         grouped_pool = ctx.enter_context(tc.tile_pool(name="grouped", bufs=4))
         codes_pool = ctx.enter_context(tc.tile_pool(name="codes", bufs=6))
         wide_pool = ctx.enter_context(tc.tile_pool(name="wide", bufs=1))
-        y_pool = ctx.enter_context(tc.tile_pool(name="y", bufs=4 * B_TILES))
+        y_pool = ctx.enter_context(tc.tile_pool(name="y", bufs=2 * B_TILES))
         psum = ctx.enter_context(tc.psum_pool(name="psum", bufs=1))
         ctx.enter_context(tc.manual_schedule())
 
@@ -158,35 +158,46 @@ def tile_lstm_peephole_build_pb_kernel(
         def parts_of(unit):
             if unit < GATE_CHUNKS:
                 return [(N_ACTS + unit, 0), (N_ACTS + unit, N_TILE)]
-            return [readout_part(unit - GATE_CHUNKS, g) for g in range(PASSES)]
+            n = unit - GATE_CHUNKS
+            pair, g = divmod(n, PASSES)
+            if pair < 2:
+                return [readout_part(pair * HALVES + half, g) for half in range(HALVES)]
+            return [readout_part(n, g) for g in range(PASSES)]
 
         grouped_of = {}
         codes_of = {}
         scales_of = {}
 
         def regroup_views(unit, s):
+            if unit not in grouped_of:
+                grouped_of[unit] = grouped_pool.tile(
+                    [P, CHUNK_ELEMS], BF16, tag="grouped", name="grouped", align_bytes=64
+                )
             j, col = parts_of(unit)[s]
             dst = grouped_of[unit][:].rearrange("p (s c r t) -> p s c t r", s=2, r=RUN, t=PACK)
             src = raws[j][:].rearrange("p (t c r) -> p c t r", t=PACK, r=RUN)
             return dst[:, s, :, :, :], src[:, col // RUN : (col + N_TILE) // RUN, :, :]
 
-        def regroup_first(unit):
-            grouped_of[unit] = grouped_pool.tile(
-                [P, CHUNK_ELEMS], BF16, tag="grouped", name="grouped", align_bytes=64
-            )
-            dst, src = regroup_views(unit, 0)
-            nc.vector.tensor_copy(out=dst, in_=src)
-
         def shared_cols(unit):
             if unit == GATE_CHUNKS:
                 return 0
+            if unit == GATE_CHUNKS + 3:
+                return N_TILE
             return GATE_SHARED_VECTOR_COLS if unit < GATE_CHUNKS else READOUT_SHARED_VECTOR_COLS
 
-        def regroup_second(unit):
-            shared = shared_cols(unit)
-            split = shared // RUN
+        def regroup_first(unit):
+            dst, src = regroup_views(unit, 0)
+            nc.vector.tensor_copy(out=dst, in_=src)
+
+        def regroup_scalar(unit):
+            split = shared_cols(unit) // RUN
             dst, src = regroup_views(unit, 1)
-            nc.scalar.copy(out=dst[:, split:, :, :], in_=src[:, split:, :, :])
+            if split < N_TILE // RUN:
+                nc.scalar.copy(out=dst[:, split:, :, :], in_=src[:, split:, :, :])
+
+        def regroup_vector(unit):
+            split = shared_cols(unit) // RUN
+            dst, src = regroup_views(unit, 1)
             if split > 0:
                 nc.vector.tensor_copy(out=dst[:, :split, :, :], in_=src[:, :split, :, :])
             if unit < 2:
@@ -194,6 +205,10 @@ def tile_lstm_peephole_build_pb_kernel(
             if unit == 1:
                 for j in range(READOUT_CHUNKS):
                     load_next()
+
+        def regroup_second(unit):
+            regroup_scalar(unit)
+            regroup_vector(unit)
 
         def regroup(unit):
             regroup_first(unit)
@@ -263,23 +278,28 @@ def tile_lstm_peephole_build_pb_kernel(
                 in_=ht_grouped[0][:, g, :],
             )
 
-        def readout_passes(n):
+        def readout_passes(blocks):
+            cols = slice(blocks[0] * N_TILE, (blocks[-1] + 1) * N_TILE)
             for i in range(B_TILES):
-                y = y_pool.tile([P, N_TILE], F32, tag="y", name="y")
-                rows = slice(i * P, (i + 1) * P)
-                acc = bank_tile(i + B_TILES * (n % HALVES), [P, N_TILE], "acc")
-                for g in range(PASSES):
-                    nc.tensor.matmul_mx(
-                        out=acc[:],
-                        lhsT=ht_codes[:, g, rows].bitcast(FP8X4),
-                        lhsT_scale=ht_scales[:, g, rows],
-                        rhs=codes_of[readout_part(n, g)],
-                        rhs_scale=scales_of[readout_part(n, g)],
-                        start=(g == 0),
-                        stop=(g == PASSES - 1),
-                    )
-                nc.scalar.activation(out=y[:], in_=acc[:], func=ACT.Sigmoid)
-                nc.sync.dma_start(out=yt_rows[:, i, n * N_TILE : (n + 1) * N_TILE], in_=y[:])
+                y = y_pool.tile([P, CHUNK_COLS], F32, tag="y", name="y")
+                for n in blocks:
+                    readout_tile(n, i, y[:, (n - blocks[0]) * N_TILE : (n - blocks[0] + 1) * N_TILE])
+                nc.sync.dma_start(out=yt_rows[:, i, cols], in_=y[:, : len(blocks) * N_TILE])
+
+        def readout_tile(n, i, y):
+            rows = slice(i * P, (i + 1) * P)
+            acc = bank_tile(i + B_TILES * (n % HALVES), [P, N_TILE], "acc")
+            for g in range(PASSES):
+                nc.tensor.matmul_mx(
+                    out=acc[:],
+                    lhsT=ht_codes[:, g, rows].bitcast(FP8X4),
+                    lhsT_scale=ht_scales[:, g, rows],
+                    rhs=codes_of[readout_part(n, g)],
+                    rhs_scale=scales_of[readout_part(n, g)],
+                    start=(g == 0),
+                    stop=(g == PASSES - 1),
+                )
+            nc.scalar.activation(out=y, in_=acc[:], func=ACT.Sigmoid)
 
         transpose(0)
         for i in range(B_TILES):
@@ -304,26 +324,35 @@ def tile_lstm_peephole_build_pb_kernel(
 
         first = GATE_CHUNKS
         regroup(first)
+        regroup_first(first + 1)
         for i in range(B_TILES):
             hidden_state(0, i)
         quantise(first)
         for i in range(B_TILES):
             hidden_state(1, i)
-        regroup(first + 1)
+        regroup_second(first + 1)
         transpose_hidden_state(0)
         transpose_hidden_state(1)
-        regroup_first(first + 2)
         quantise_hidden_state(0)
-        quantise_hidden_state(1)
-        for i in range(B_TILES):
-            nc.sync.dma_start(out=ht_rows[:, i, :], in_=tanh_c[:, i, :])
         quantise(first + 1)
-        regroup_second(first + 2)
-        for n in range(N_BLOCKS):
-            readout_passes(n)
-            if n + 3 < N_BLOCKS:
-                regroup_first(first + n + 3)
-            if n + 2 < N_BLOCKS:
-                quantise(first + n + 2)
-            if n + 3 < N_BLOCKS:
-                regroup_second(first + n + 3)
+        quantise_hidden_state(1)
+        nc.sync.dma_start(out=ht_rows, in_=tanh_c[:])
+        regroup(first + 2)
+        readout_passes([0, 1])
+        quantise(first + 2)
+        regroup(first + 3)
+        regroup_first(first + 4)
+        quantise(first + 3)
+        for n in range(4, 6):
+            regroup_scalar(first + n)
+        readout_passes([2, 3])
+        regroup_vector(first + 4)
+        for n in range(4, N_BLOCKS):
+            if n + 1 < N_BLOCKS:
+                regroup_first(first + n + 1)
+            quantise(first + n)
+            if n + 1 < N_BLOCKS:
+                if n + 1 >= 6:
+                    regroup_scalar(first + n + 1)
+                regroup_vector(first + n + 1)
+            readout_passes([n])

@@ -27,7 +27,6 @@ RUN = 4
 N_ACTS = 3
 GATE_CHUNKS = N_ACTS * PASSES
 READOUT_COLS = ((0, 1024), (1024, 4096))
-READOUT_CHUNKS = PASSES * len(READOUT_COLS)
 
 N_BLOCKS = VOCAB // N_TILE
 UNITS = GATE_CHUNKS + N_BLOCKS
@@ -35,7 +34,7 @@ UNITS = GATE_CHUNKS + N_BLOCKS
 GATE_SHARED_VECTOR_COLS = 64
 READOUT_SHARED_VECTOR_COLS = 416
 
-RAW_BUFS = 4
+SLOTS = N_ACTS + GATE_CHUNKS + PASSES
 
 FLOPS = 2 * BATCH * HIDDEN * (N_ACTS * HIDDEN + VOCAB)
 
@@ -62,11 +61,10 @@ def tile_lstm_peephole_build_pb_kernel(
     with ExitStack() as ctx:
         const = ctx.enter_context(tc.tile_pool(name="const", bufs=1))
         keep = ctx.enter_context(tc.tile_pool(name="keep", bufs=1))
-        raw_pool = ctx.enter_context(tc.tile_pool(name="raw", bufs=RAW_BUFS))
+        slots = ctx.enter_context(tc.tile_pool(name="slots", bufs=SLOTS))
         grouped_pool = ctx.enter_context(tc.tile_pool(name="grouped", bufs=4))
         codes_pool = ctx.enter_context(tc.tile_pool(name="codes", bufs=6))
-        wide_pool = ctx.enter_context(tc.tile_pool(name="wide", bufs=1))
-        y_pool = ctx.enter_context(tc.tile_pool(name="y", bufs=2 * B_TILES))
+        wide_pool = ctx.enter_context(tc.tile_pool(name="wide", bufs=PASSES))
         psum = ctx.enter_context(tc.psum_pool(name="psum", bufs=1))
         ctx.enter_context(tc.manual_schedule())
 
@@ -76,14 +74,11 @@ def tile_lstm_peephole_build_pb_kernel(
         raws = {}
 
         def load(j, first):
-            if j == 0:
-                raw = keep.tile([P, CHUNK_ELEMS], BF16, tag="c", name="raw")
-            elif j < N_ACTS + GATE_CHUNKS:
-                raw = raw_pool.tile([P, CHUNK_ELEMS], BF16, tag="raw")
+            runs, width = sources[j].shape[1:]
+            if runs * width <= CHUNK_ELEMS:
+                raw = slots.tile([P, CHUNK_ELEMS], BF16, tag="slot", name="raw")
             else:
-                cols = sources[j].shape[2]
-                raw = wide_pool.tile([P, PACK * cols], BF16, tag="wide" + str(j), name="raw")
-            runs = sources[j].shape[1]
+                raw = wide_pool.tile([P, runs * width], BF16, tag="wide", name="raw")
             dst = raw[:].rearrange("p (r m) -> p r m", r=runs)
             step = 1 if first else runs
             for r in range(0, runs, step):
@@ -99,7 +94,7 @@ def tile_lstm_peephole_build_pb_kernel(
             load(load_order[len(loaded)], first=(len(loaded) == 0))
             loaded.append(True)
 
-        for j in range(RAW_BUFS + 1):
+        for j in range(len(sources)):
             load_next()
 
         ident = const.tile([P, P], F32)
@@ -133,8 +128,6 @@ def tile_lstm_peephole_build_pb_kernel(
                 else:
                     nc.vector.tensor_copy(out=dst, in_=src)
             grouped_act[a] = grouped
-            if a > 0:
-                load_next()
 
         def quantise_act(a):
             nc.vector.quantize_mx(
@@ -200,11 +193,6 @@ def tile_lstm_peephole_build_pb_kernel(
             dst, src = regroup_views(unit, 1)
             if split > 0:
                 nc.vector.tensor_copy(out=dst[:, :split, :, :], in_=src[:, :split, :, :])
-            if unit < 2:
-                load_next()
-            if unit == 1:
-                for j in range(READOUT_CHUNKS):
-                    load_next()
 
         def regroup_second(unit):
             regroup_scalar(unit)
@@ -248,11 +236,15 @@ def tile_lstm_peephole_build_pb_kernel(
         ht_codes = keep.tile([P, PASSES, B_TILES * P], U32, align_bytes=64)
         ht_scales = keep.tile([P, PASSES, B_TILES * P], U8, align_bytes=64)
 
+        sigs = {}
+
         def hidden_state(g, i):
-            sig = y_pool.tile([P, N_TILE], F32, tag="y", name="sig")
-            nc.scalar.activation(out=sig[:], in_=zo[(i, g)][:], func=ACT.Sigmoid)
+            if i == 0:
+                sigs[g] = slots.tile([P, B_TILES, N_TILE], F32, tag="slot", name="sig")
+            sig = sigs[g][:, i, :]
+            nc.scalar.activation(out=sig, in_=zo[(i, g)][:], func=ACT.Sigmoid)
             ht = tanh_c[:, i, g * K_PASS : (g + 1) * K_PASS]
-            nc.vector.tensor_mul(out=ht, in0=sig[:], in1=ht)
+            nc.vector.tensor_mul(out=ht, in0=sig, in1=ht)
 
         ht_grouped = []
 
@@ -281,7 +273,7 @@ def tile_lstm_peephole_build_pb_kernel(
         def readout_passes(blocks):
             cols = slice(blocks[0] * N_TILE, (blocks[-1] + 1) * N_TILE)
             for i in range(B_TILES):
-                y = y_pool.tile([P, CHUNK_COLS], F32, tag="y", name="y")
+                y = slots.tile([P, CHUNK_COLS], F32, tag="slot", name="y")
                 for n in blocks:
                     readout_tile(n, i, y[:, (n - blocks[0]) * N_TILE : (n - blocks[0] + 1) * N_TILE])
                 nc.sync.dma_start(out=yt_rows[:, i, cols], in_=y[:, : len(blocks) * N_TILE])

@@ -31,7 +31,7 @@ READOUT_COLS = ((0, 1024), (1024, 4096))
 N_BLOCKS = VOCAB // N_TILE
 UNITS = GATE_CHUNKS + N_BLOCKS
 
-GATE_SHARED_VECTOR_COLS = 64
+GATE_SHARED_VECTOR_COLS = 32
 READOUT_SHARED_VECTOR_COLS = 416
 
 SLOTS = N_ACTS + GATE_CHUNKS + PASSES
@@ -71,6 +71,13 @@ def tile_lstm_peephole_build_pb_kernel(
         def bank_tile(b, shape, name):
             return psum.tile(shape, F32, tag="bank" + str(b), name=name)
 
+        def keep_clock(b, count):
+            idle = bank_tile(b, [P, N_TILE], "idle")
+            for k in range(count):
+                nc.tensor.matmul(
+                    idle[:], lhsT=zeros[:, :P], rhs=zeros[:], start=True, stop=True
+                )
+
         raws = {}
 
         def load(j, first):
@@ -99,6 +106,8 @@ def tile_lstm_peephole_build_pb_kernel(
 
         ident = const.tile([P, P], F32)
         make_identity(nc, ident[:])
+        zeros = const.tile([P, N_TILE], BF16)
+        nc.gpsimd.memset(zeros[:], 0.0)
 
         warm = const.tile([P, 1], F32)
         nc.vector.memset(warm[:], 0.0)
@@ -298,6 +307,7 @@ def tile_lstm_peephole_build_pb_kernel(
             tanh_tile(i)
         quantise_act(0)
         regroup(0)
+        keep_clock(7, 4)
         transpose(1)
         quantise(0)
         transpose(2)
@@ -317,12 +327,13 @@ def tile_lstm_peephole_build_pb_kernel(
         first = GATE_CHUNKS
         regroup(first)
         regroup_first(first + 1)
+        regroup_vector(first + 1)
         for i in range(B_TILES):
             hidden_state(0, i)
         quantise(first)
         for i in range(B_TILES):
             hidden_state(1, i)
-        regroup_second(first + 1)
+        regroup_scalar(first + 1)
         transpose_hidden_state(0)
         transpose_hidden_state(1)
         quantise_hidden_state(0)
@@ -331,6 +342,7 @@ def tile_lstm_peephole_build_pb_kernel(
         nc.sync.dma_start(out=ht_rows, in_=tanh_c[:])
         regroup(first + 2)
         readout_passes([0, 1])
+        keep_clock(0, 4)
         quantise(first + 2)
         regroup(first + 3)
         regroup_first(first + 4)

@@ -26,7 +26,13 @@ RUN = 4
 
 N_ACTS = 3
 GATE_CHUNKS = N_ACTS * PASSES
-READOUT_COLS = ((0, 1024), (1024, 4096))
+READOUT_CHUNKS = (
+    (0, 0, 1024),
+    (1, 0, 1024),
+    (0, 1024, 4096),
+    (1, 1024, 2048),
+    (1, 2048, 4096),
+)
 
 N_BLOCKS = VOCAB // N_TILE
 UNITS = GATE_CHUNKS + N_BLOCKS
@@ -34,7 +40,7 @@ UNITS = GATE_CHUNKS + N_BLOCKS
 GATE_SHARED_VECTOR_COLS = 32
 READOUT_SHARED_VECTOR_COLS = 416
 
-SLOTS = N_ACTS + GATE_CHUNKS + PASSES
+SLOTS = N_ACTS + GATE_CHUNKS + PASSES + 1
 
 FLOPS = 2 * BATCH * HIDDEN * (N_ACTS * HIDDEN + VOCAB)
 
@@ -53,10 +59,9 @@ def tile_lstm_peephole_build_pb_kernel(
         for g in range(PASSES):
             rows = weight[g * K_PASS : (g + 1) * K_PASS, :]
             sources.append(rows.rearrange("(u q e) n -> q u (e n)", u=2, e=2))
-    for low, high in READOUT_COLS:
-        for g in range(PASSES):
-            rows = w_op[g * K_PASS : (g + 1) * K_PASS, low:high]
-            sources.append(rows.rearrange("(t p) n -> p t n", p=P))
+    for g, low, high in READOUT_CHUNKS:
+        rows = w_op[g * K_PASS : (g + 1) * K_PASS, low:high]
+        sources.append(rows.rearrange("(t p) n -> p t n", p=P))
 
     with ExitStack() as ctx:
         const = ctx.enter_context(tc.tile_pool(name="const", bufs=1))
@@ -64,7 +69,7 @@ def tile_lstm_peephole_build_pb_kernel(
         slots = ctx.enter_context(tc.tile_pool(name="slots", bufs=SLOTS))
         grouped_pool = ctx.enter_context(tc.tile_pool(name="grouped", bufs=4))
         codes_pool = ctx.enter_context(tc.tile_pool(name="codes", bufs=6))
-        wide_pool = ctx.enter_context(tc.tile_pool(name="wide", bufs=PASSES))
+        wide_pool = ctx.enter_context(tc.tile_pool(name="wide", bufs=1))
         psum = ctx.enter_context(tc.psum_pool(name="psum", bufs=1))
         ctx.enter_context(tc.manual_schedule())
 
@@ -85,7 +90,7 @@ def tile_lstm_peephole_build_pb_kernel(
             if runs * width <= CHUNK_ELEMS:
                 raw = slots.tile([P, CHUNK_ELEMS], BF16, tag="slot", name="raw")
             else:
-                raw = wide_pool.tile([P, runs * width], BF16, tag="wide", name="raw")
+                raw = wide_pool.tile([P, runs * width], BF16, tag="wide" + str(j), name="raw")
             dst = raw[:].rearrange("p (r m) -> p r m", r=runs)
             step = 1 if first else runs
             for r in range(0, runs, step):
@@ -153,16 +158,16 @@ def tile_lstm_peephole_build_pb_kernel(
             )
 
         def readout_part(n, g):
-            for block, (low, high) in enumerate(READOUT_COLS):
-                if low <= n * N_TILE < high:
-                    return N_ACTS + GATE_CHUNKS + block * PASSES + g, n * N_TILE - low
+            for j, (chunk_g, low, high) in enumerate(READOUT_CHUNKS):
+                if g == chunk_g and low <= n * N_TILE < high:
+                    return N_ACTS + GATE_CHUNKS + j, n * N_TILE - low
 
         def parts_of(unit):
             if unit < GATE_CHUNKS:
                 return [(N_ACTS + unit, 0), (N_ACTS + unit, N_TILE)]
             n = unit - GATE_CHUNKS
             pair, g = divmod(n, PASSES)
-            if pair < 2:
+            if pair < 1:
                 return [readout_part(pair * HALVES + half, g) for half in range(HALVES)]
             return [readout_part(n, g) for g in range(PASSES)]
 
@@ -183,8 +188,6 @@ def tile_lstm_peephole_build_pb_kernel(
         def shared_cols(unit):
             if unit == GATE_CHUNKS:
                 return 0
-            if unit == GATE_CHUNKS + 3:
-                return N_TILE
             return GATE_SHARED_VECTOR_COLS if unit < GATE_CHUNKS else READOUT_SHARED_VECTOR_COLS
 
         def regroup_first(unit):
@@ -341,22 +344,19 @@ def tile_lstm_peephole_build_pb_kernel(
         quantise_hidden_state(1)
         nc.sync.dma_start(out=ht_rows, in_=tanh_c[:])
         regroup(first + 2)
+        regroup_scalar(first + 3)
         readout_passes([0, 1])
-        keep_clock(0, 4)
+        regroup_first(first + 3)
         quantise(first + 2)
-        regroup(first + 3)
-        regroup_first(first + 4)
-        quantise(first + 3)
-        for n in range(4, 6):
-            regroup_scalar(first + n)
-        readout_passes([2, 3])
-        regroup_vector(first + 4)
-        for n in range(4, N_BLOCKS):
-            if n + 1 < N_BLOCKS:
-                regroup_first(first + n + 1)
-            quantise(first + n)
-            if n + 1 < N_BLOCKS:
-                if n + 1 >= 6:
-                    regroup_scalar(first + n + 1)
-                regroup_vector(first + n + 1)
+        regroup_vector(first + 3)
+        keep_clock(0, 3)
+        for n in range(2, N_BLOCKS):
+            if n + 2 < N_BLOCKS:
+                regroup_scalar(first + n + 2)
             readout_passes([n])
+            if n + 2 < N_BLOCKS:
+                regroup_first(first + n + 2)
+            if n + 1 < N_BLOCKS:
+                quantise(first + n + 1)
+            if n + 2 < N_BLOCKS:
+                regroup_vector(first + n + 2)

@@ -42,6 +42,8 @@ READOUT_SHARED_VECTOR_COLS = 416
 
 SLOTS = N_ACTS + GATE_CHUNKS + PASSES + 1
 
+LAST_UNIT = GATE_CHUNKS + N_BLOCKS - 1
+
 FLOPS = 2 * BATCH * HIDDEN * (N_ACTS * HIDDEN + VOCAB)
 
 
@@ -92,9 +94,14 @@ def tile_lstm_peephole_build_pb_kernel(
             else:
                 raw = wide_pool.tile([P, runs * width], BF16, tag="wide" + str(j), name="raw")
             dst = raw[:].rearrange("p (r m) -> p r m", r=runs)
-            step = 1 if first else runs
+            step = 1 if first else (2 if j < N_ACTS else runs)
             for r in range(0, runs, step):
-                nc.sync.dma_start(out=dst[:, r : r + step, :], in_=sources[j][:, r : r + step, :])
+                cut = width // 2 if first and r == 0 else width
+                for low in range(0, width, cut):
+                    nc.sync.dma_start(
+                        out=dst[:, r : r + step, low : low + cut],
+                        in_=sources[j][:, r : r + step, low : low + cut],
+                    )
             raws[j] = raw
 
         loaded = []
@@ -151,11 +158,14 @@ def tile_lstm_peephole_build_pb_kernel(
             )
 
         def tanh_tile(i):
-            nc.scalar.activation(
-                out=tanh_c[:, i, :],
-                in_=raws[0][:, i * HIDDEN : (i + 1) * HIDDEN],
-                func=ACT.Tanh,
-            )
+            cut = HIDDEN // 2 if i == 0 else HIDDEN
+            for low in range(0, HIDDEN, cut):
+                begin = i * HIDDEN + low
+                nc.scalar.activation(
+                    out=tanh_c[:, i, low : low + cut],
+                    in_=raws[0][:, begin : begin + cut],
+                    func=ACT.Tanh,
+                )
 
         def readout_part(n, g):
             for j, (chunk_g, low, high) in enumerate(READOUT_CHUNKS):
@@ -166,6 +176,10 @@ def tile_lstm_peephole_build_pb_kernel(
             if unit < GATE_CHUNKS:
                 return [(N_ACTS + unit, 0), (N_ACTS + unit, N_TILE)]
             n = unit - GATE_CHUNKS
+            if unit >= LAST_UNIT:
+                half = (unit - LAST_UNIT) * (N_TILE // 2)
+                last = [readout_part(N_BLOCKS - 1, g) for g in range(PASSES)]
+                return [(j, col + half) for j, col in last]
             pair, g = divmod(n, PASSES)
             if pair < 1:
                 return [readout_part(pair * HALVES + half, g) for half in range(HALVES)]
@@ -175,19 +189,26 @@ def tile_lstm_peephole_build_pb_kernel(
         codes_of = {}
         scales_of = {}
 
+        def width_of(unit):
+            return N_TILE // 2 if unit >= LAST_UNIT else N_TILE
+
         def regroup_views(unit, s):
             if unit not in grouped_of:
                 grouped_of[unit] = grouped_pool.tile(
                     [P, CHUNK_ELEMS], BF16, tag="grouped", name="grouped", align_bytes=64
                 )
             j, col = parts_of(unit)[s]
-            dst = grouped_of[unit][:].rearrange("p (s c r t) -> p s c t r", s=2, r=RUN, t=PACK)
+            width = width_of(unit)
+            flat = grouped_of[unit][:, : 2 * width * PACK]
+            dst = flat.rearrange("p (s c r t) -> p s c t r", s=2, r=RUN, t=PACK)
             src = raws[j][:].rearrange("p (t c r) -> p c t r", t=PACK, r=RUN)
-            return dst[:, s, :, :, :], src[:, col // RUN : (col + N_TILE) // RUN, :, :]
+            return dst[:, s, :, :, :], src[:, col // RUN : (col + width) // RUN, :, :]
 
         def shared_cols(unit):
             if unit == GATE_CHUNKS:
                 return 0
+            if unit >= LAST_UNIT:
+                return width_of(unit)
             return GATE_SHARED_VECTOR_COLS if unit < GATE_CHUNKS else READOUT_SHARED_VECTOR_COLS
 
         def regroup_first(unit):
@@ -197,7 +218,7 @@ def tile_lstm_peephole_build_pb_kernel(
         def regroup_scalar(unit):
             split = shared_cols(unit) // RUN
             dst, src = regroup_views(unit, 1)
-            if split < N_TILE // RUN:
+            if split < width_of(unit) // RUN:
                 nc.scalar.copy(out=dst[:, split:, :, :], in_=src[:, split:, :, :])
 
         def regroup_vector(unit):
@@ -215,12 +236,13 @@ def tile_lstm_peephole_build_pb_kernel(
             regroup_second(unit)
 
         def quantise(unit):
-            codes = codes_pool.tile([P, 2, N_TILE], U32, tag="codes", align_bytes=64)
-            scales = codes_pool.tile([P, 2, N_TILE], U8, tag="scales", align_bytes=64)
+            width = width_of(unit)
+            codes = codes_pool.tile([P, 2, width], U32, tag="codes", align_bytes=64)
+            scales = codes_pool.tile([P, 2, width], U8, tag="scales", align_bytes=64)
             nc.vector.quantize_mx(
                 out=codes[:].rearrange("p s n -> p (s n)").bitcast(FP8X4),
                 scales=scales[:].rearrange("p s n -> p (s n)"),
-                in_=grouped_of[unit][:],
+                in_=grouped_of[unit][:, : 2 * width * PACK],
             )
             for s, part in enumerate(parts_of(unit)):
                 codes_of[part] = codes[:, s, :].bitcast(FP8X4)
@@ -290,16 +312,27 @@ def tile_lstm_peephole_build_pb_kernel(
                     readout_tile(n, i, y[:, (n - blocks[0]) * N_TILE : (n - blocks[0] + 1) * N_TILE])
                 nc.sync.dma_start(out=yt_rows[:, i, cols], in_=y[:, : len(blocks) * N_TILE])
 
-        def readout_tile(n, i, y):
+        def readout_last(half):
+            width = N_TILE // 2
+            begin = VOCAB - N_TILE + half * width
+            for i in range(B_TILES):
+                y = slots.tile([P, width], F32, tag="slot", name="y")
+                readout_tile(N_BLOCKS - 1, i, y[:], half * width)
+                nc.sync.dma_start(out=yt_rows[:, i, begin : begin + width], in_=y[:])
+
+        def readout_tile(n, i, y, begin=0):
             rows = slice(i * P, (i + 1) * P)
-            acc = bank_tile(i + B_TILES * (n % HALVES), [P, N_TILE], "acc")
+            width = y.shape[1]
+            bank = i + B_TILES * ((n + begin // width) % HALVES)
+            acc = bank_tile(bank, [P, width], "acc")
+            parts = [(j, col + begin) for j, col in [readout_part(n, g) for g in range(PASSES)]]
             for g in range(PASSES):
                 nc.tensor.matmul_mx(
                     out=acc[:],
                     lhsT=ht_codes[:, g, rows].bitcast(FP8X4),
                     lhsT_scale=ht_scales[:, g, rows],
-                    rhs=codes_of[readout_part(n, g)],
-                    rhs_scale=scales_of[readout_part(n, g)],
+                    rhs=codes_of[parts[g]],
+                    rhs_scale=scales_of[parts[g]],
                     start=(g == 0),
                     stop=(g == PASSES - 1),
                 )
@@ -339,24 +372,30 @@ def tile_lstm_peephole_build_pb_kernel(
         regroup_scalar(first + 1)
         transpose_hidden_state(0)
         transpose_hidden_state(1)
-        quantise_hidden_state(0)
+        keep_clock(0, 3)
         quantise(first + 1)
+        quantise_hidden_state(0)
+        regroup_first(first + 2)
         quantise_hidden_state(1)
         nc.sync.dma_start(out=ht_rows, in_=tanh_c[:])
-        regroup(first + 2)
+        regroup_second(first + 2)
         regroup_scalar(first + 3)
         readout_passes([0, 1])
         regroup_first(first + 3)
         quantise(first + 2)
         regroup_vector(first + 3)
         keep_clock(0, 3)
-        for n in range(2, N_BLOCKS):
-            if n + 2 < N_BLOCKS:
+        for n in range(2, N_BLOCKS + 1):
+            ahead = n + 2 < N_BLOCKS + 1
+            if ahead:
                 regroup_scalar(first + n + 2)
-            readout_passes([n])
-            if n + 2 < N_BLOCKS:
+            if n < N_BLOCKS - 1:
+                readout_passes([n])
+            else:
+                readout_last(n - N_BLOCKS + 1)
+            if ahead:
                 regroup_first(first + n + 2)
-            if n + 1 < N_BLOCKS:
+            if n < N_BLOCKS:
                 quantise(first + n + 1)
-            if n + 2 < N_BLOCKS:
+            if ahead:
                 regroup_vector(first + n + 2)

from contextlib import ExitStack

import concourse.mybir as mybir
from concourse.masks import make_identity

F32 = mybir.dt.float32
BF16 = mybir.dt.bfloat16
U32 = mybir.dt.uint32
U8 = mybir.dt.uint8
FP8X4 = mybir.dt.float8_e4m3fn_x4
ACT = mybir.ActivationFunctionType

P = 128
PACK = 4
K_PASS = P * PACK
BATCH = 512
HIDDEN = 1024
VOCAB = 4096
B_TILES = BATCH // P
PASSES = HIDDEN // K_PASS
N_TILE = 512
CHUNK_COLS = 1024
CHUNK_ELEMS = PACK * CHUNK_COLS
HALVES = CHUNK_COLS // N_TILE
RUN = 4

N_ACTS = 3
GATE_CHUNKS = N_ACTS * PASSES
READOUT_CHUNKS = (
    (0, 0, 1024),
    (1, 0, 1024),
    (0, 1024, 4096),
    (1, 1024, 2048),
    (1, 2048, 4096),
)

N_BLOCKS = VOCAB // N_TILE
UNITS = GATE_CHUNKS + N_BLOCKS

GATE_SHARED_VECTOR_COLS = 32
READOUT_SHARED_VECTOR_COLS = 416

SLOTS = N_ACTS + GATE_CHUNKS + PASSES + 1

LAST_UNIT = GATE_CHUNKS + N_BLOCKS - 1

FLOPS = 2 * BATCH * HIDDEN * (N_ACTS * HIDDEN + VOCAB)


def tile_lstm_peephole_build_pb_kernel(
    tc, input_data, previous_hidden_state, c_t, w_ip_o, w_output, w_output_c, w_op, out_0, out_1
):
    nc = tc.nc
    yt_rows = out_0.rearrange("(p i) n -> p i n", i=B_TILES)
    ht_rows = out_1.rearrange("(p i) n -> p i n", i=B_TILES)

    sources = []
    for act in (c_t, input_data, previous_hidden_state):
        sources.append(act.rearrange("(p i) k -> p i k", i=B_TILES))
    for weight in (w_output_c, w_ip_o, w_output):
        for g in range(PASSES):
            rows = weight[g * K_PASS : (g + 1) * K_PASS, :]
            sources.append(rows.rearrange("(u q e) n -> q u (e n)", u=2, e=2))
    for g, low, high in READOUT_CHUNKS:
        rows = w_op[g * K_PASS : (g + 1) * K_PASS, low:high]
        sources.append(rows.rearrange("(t p) n -> p t n", p=P))

    with ExitStack() as ctx:
        const = ctx.enter_context(tc.tile_pool(name="const", bufs=1))
        keep = ctx.enter_context(tc.tile_pool(name="keep", bufs=1))
        slots = ctx.enter_context(tc.tile_pool(name="slots", bufs=SLOTS))
        grouped_pool = ctx.enter_context(tc.tile_pool(name="grouped", bufs=4))
        codes_pool = ctx.enter_context(tc.tile_pool(name="codes", bufs=6))
        wide_pool = ctx.enter_context(tc.tile_pool(name="wide", bufs=1))
        psum = ctx.enter_context(tc.psum_pool(name="psum", bufs=1))
        ctx.enter_context(tc.manual_schedule())

        def bank_tile(b, shape, name):
            return psum.tile(shape, F32, tag="bank" + str(b), name=name)

        def keep_clock(b, count):
            idle = bank_tile(b, [P, N_TILE], "idle")
            for k in range(count):
                nc.tensor.matmul(
                    idle[:], lhsT=zeros[:, :P], rhs=zeros[:], start=True, stop=True
                )

        raws = {}

        def load(j, first):
            runs, width = sources[j].shape[1:]
            if runs * width <= CHUNK_ELEMS:
                raw = slots.tile([P, CHUNK_ELEMS], BF16, tag="slot", name="raw")
            else:
                raw = wide_pool.tile([P, runs * width], BF16, tag="wide" + str(j), name="raw")
            dst = raw[:].rearrange("p (r m) -> p r m", r=runs)
            step = 1 if first else (2 if j < N_ACTS else runs)
            for r in range(0, runs, step):
                cut = width // 2 if first and r == 0 else width
                for low in range(0, width, cut):
                    nc.sync.dma_start(
                        out=dst[:, r : r + step, low : low + cut],
                        in_=sources[j][:, r : r + step, low : low + cut],
                    )
            raws[j] = raw

        loaded = []

        load_order = list(range(len(sources)))
        load_order[1 : N_ACTS + 1] = [N_ACTS, 1, 2]

        def load_next():
            load(load_order[len(loaded)], first=(len(loaded) == 0))
            loaded.append(True)

        for j in range(len(sources)):
            load_next()

        ident = const.tile([P, P], F32)
        make_identity(nc, ident[:])
        zeros = const.tile([P, N_TILE], BF16)
        nc.gpsimd.memset(zeros[:], 0.0)

        warm = const.tile([P, 1], F32)
        nc.vector.memset(warm[:], 0.0)
        nc.scalar.activation(out=warm[:], in_=warm[:], func=ACT.Sigmoid)

        act_codes = keep.tile([P, N_ACTS, B_TILES * PASSES * P], U32, align_bytes=64)
        act_scales = keep.tile([P, N_ACTS, B_TILES * PASSES * P], U8, align_bytes=64)
        tanh_c = keep.tile([P, B_TILES, HIDDEN], F32)

        grouped_act = {}

        def transpose(a):
            words = raws[a][:].bitcast(F32)
            grouped = grouped_pool.tile([P, CHUNK_ELEMS], BF16, tag="grouped", align_bytes=64)
            grouped_words = grouped[:].bitcast(F32)
            words_per_tile = HIDDEN // 2
            for i in range(B_TILES):
                bank = bank_tile(i + (B_TILES if a > 0 else 0), [P, PASSES * 2, P], "bank")
                for w in range(PASSES * 2):
                    first = i * words_per_tile + w * P
                    nc.tensor.transpose(bank[:, w, :], words[:, first : first + P], ident[:])
                dst = grouped_words[:, i * words_per_tile : (i + 1) * words_per_tile]
                dst = dst.rearrange("p (g b u) -> p g b u", g=PASSES, u=2)
                src = bank[:].rearrange("p (g u) b -> p g b u", u=2)
                if a > 0:
                    nc.scalar.copy(out=dst, in_=src)
                else:
                    nc.vector.tensor_copy(out=dst, in_=src)
            grouped_act[a] = grouped

        def quantise_act(a):
            nc.vector.quantize_mx(
                out=act_codes[:, a, :].bitcast(FP8X4),
                scales=act_scales[:, a, :],
                in_=grouped_act[a][:],
            )

        def tanh_tile(i):
            cut = HIDDEN // 2 if i == 0 else HIDDEN
            for low in range(0, HIDDEN, cut):
                begin = i * HIDDEN + low
                nc.scalar.activation(
                    out=tanh_c[:, i, low : low + cut],
                    in_=raws[0][:, begin : begin + cut],
                    func=ACT.Tanh,
                )

        def readout_part(n, g):
            for j, (chunk_g, low, high) in enumerate(READOUT_CHUNKS):
                if g == chunk_g and low <= n * N_TILE < high:
                    return N_ACTS + GATE_CHUNKS + j, n * N_TILE - low

        def parts_of(unit):
            if unit < GATE_CHUNKS:
                return [(N_ACTS + unit, 0), (N_ACTS + unit, N_TILE)]
            n = unit - GATE_CHUNKS
            if unit >= LAST_UNIT:
                half = (unit - LAST_UNIT) * (N_TILE // 2)
                last = [readout_part(N_BLOCKS - 1, g) for g in range(PASSES)]
                return [(j, col + half) for j, col in last]
            pair, g = divmod(n, PASSES)
            if pair < 1:
                return [readout_part(pair * HALVES + half, g) for half in range(HALVES)]
            return [readout_part(n, g) for g in range(PASSES)]

        grouped_of = {}
        codes_of = {}
        scales_of = {}

        def width_of(unit):
            return N_TILE // 2 if unit >= LAST_UNIT else N_TILE

        def regroup_views(unit, s):
            if unit not in grouped_of:
                grouped_of[unit] = grouped_pool.tile(
                    [P, CHUNK_ELEMS], BF16, tag="grouped", name="grouped", align_bytes=64
                )
            j, col = parts_of(unit)[s]
            width = width_of(unit)
            flat = grouped_of[unit][:, : 2 * width * PACK]
            dst = flat.rearrange("p (s c r t) -> p s c t r", s=2, r=RUN, t=PACK)
            src = raws[j][:].rearrange("p (t c r) -> p c t r", t=PACK, r=RUN)
            return dst[:, s, :, :, :], src[:, col // RUN : (col + width) // RUN, :, :]

        def shared_cols(unit):
            if unit == GATE_CHUNKS:
                return 0
            if unit >= LAST_UNIT:
                return width_of(unit)
            return GATE_SHARED_VECTOR_COLS if unit < GATE_CHUNKS else READOUT_SHARED_VECTOR_COLS

        def regroup_first(unit):
            dst, src = regroup_views(unit, 0)
            nc.vector.tensor_copy(out=dst, in_=src)

        def regroup_scalar(unit):
            split = shared_cols(unit) // RUN
            dst, src = regroup_views(unit, 1)
            if split < width_of(unit) // RUN:
                nc.scalar.copy(out=dst[:, split:, :, :], in_=src[:, split:, :, :])

        def regroup_vector(unit):
            split = shared_cols(unit) // RUN
            dst, src = regroup_views(unit, 1)
            if split > 0:
                nc.vector.tensor_copy(out=dst[:, :split, :, :], in_=src[:, :split, :, :])

        def regroup_second(unit):
            regroup_scalar(unit)
            regroup_vector(unit)

        def regroup(unit):
            regroup_first(unit)
            regroup_second(unit)

        def quantise(unit):
            width = width_of(unit)
            codes = codes_pool.tile([P, 2, width], U32, tag="codes", align_bytes=64)
            scales = codes_pool.tile([P, 2, width], U8, tag="scales", align_bytes=64)
            nc.vector.quantize_mx(
                out=codes[:].rearrange("p s n -> p (s n)").bitcast(FP8X4),
                scales=scales[:].rearrange("p s n -> p (s n)"),
                in_=grouped_of[unit][:, : 2 * width * PACK],
            )
            for s, part in enumerate(parts_of(unit)):
                codes_of[part] = codes[:, s, :].bitcast(FP8X4)
                scales_of[part] = scales[:, s, :]

        zo = {}

        def gate_passes(j, halves=range(HALVES)):
            a, g = divmod(j, PASSES)
            for half in halves:
                for i in range(B_TILES):
                    if j == 0:
                        zo[(i, half)] = bank_tile(i + B_TILES * half, [P, N_TILE], "zo")
                    rows = slice((i * PASSES + g) * P, (i * PASSES + g + 1) * P)
                    nc.tensor.matmul_mx(
                        out=zo[(i, half)][:],
                        lhsT=act_codes[:, a, rows].bitcast(FP8X4),
                        lhsT_scale=act_scales[:, a, rows],
                        rhs=codes_of[(N_ACTS + j, half * N_TILE)],
                        rhs_scale=scales_of[(N_ACTS + j, half * N_TILE)],
                        start=(j == 0),
                        stop=(j == GATE_CHUNKS - 1),
                    )

        ht_codes = keep.tile([P, PASSES, B_TILES * P], U32, align_bytes=64)
        ht_scales = keep.tile([P, PASSES, B_TILES * P], U8, align_bytes=64)

        sigs = {}

        def hidden_state(g, i):
            if i == 0:
                sigs[g] = slots.tile([P, B_TILES, N_TILE], F32, tag="slot", name="sig")
            sig = sigs[g][:, i, :]
            nc.scalar.activation(out=sig, in_=zo[(i, g)][:], func=ACT.Sigmoid)
            ht = tanh_c[:, i, g * K_PASS : (g + 1) * K_PASS]
            nc.vector.tensor_mul(out=ht, in0=sig, in1=ht)

        ht_grouped = []

        def transpose_hidden_state(g):
            if g == 0:
                tile = grouped_pool.tile([P, CHUNK_ELEMS], BF16, tag="grouped", align_bytes=64)
                ht_grouped.append(tile[:].rearrange("p (g m) -> p g m", g=PASSES))
            for i in range(B_TILES):
                bank = bank_tile(i + B_TILES * g, [P, PACK, P], "bank")
                for t in range(PACK):
                    first = g * K_PASS + t * P
                    nc.tensor.transpose(bank[:, t, :], tanh_c[:, i, first : first + P], ident[:])
                dst = ht_grouped[0][:, g, i * K_PASS : (i + 1) * K_PASS]
                nc.scalar.copy(
                    out=dst.rearrange("p (b t) -> p b t", t=PACK),
                    in_=bank[:].rearrange("p t b -> p b t"),
                )

        def quantise_hidden_state(g):
            nc.vector.quantize_mx(
                out=ht_codes[:, g, :].bitcast(FP8X4),
                scales=ht_scales[:, g, :],
                in_=ht_grouped[0][:, g, :],
            )

        def readout_passes(blocks):
            cols = slice(blocks[0] * N_TILE, (blocks[-1] + 1) * N_TILE)
            for i in range(B_TILES):
                y = slots.tile([P, CHUNK_COLS], F32, tag="slot", name="y")
                for n in blocks:
                    readout_tile(n, i, y[:, (n - blocks[0]) * N_TILE : (n - blocks[0] + 1) * N_TILE])
                nc.sync.dma_start(out=yt_rows[:, i, cols], in_=y[:, : len(blocks) * N_TILE])

        def readout_last(half):
            width = N_TILE // 2
            begin = VOCAB - N_TILE + half * width
            for i in range(B_TILES):
                y = slots.tile([P, width], F32, tag="slot", name="y")
                readout_tile(N_BLOCKS - 1, i, y[:], half * width)
                nc.sync.dma_start(out=yt_rows[:, i, begin : begin + width], in_=y[:])

        def readout_tile(n, i, y, begin=0):
            rows = slice(i * P, (i + 1) * P)
            width = y.shape[1]
            bank = i + B_TILES * ((n + begin // width) % HALVES)
            acc = bank_tile(bank, [P, width], "acc")
            parts = [(j, col + begin) for j, col in [readout_part(n, g) for g in range(PASSES)]]
            for g in range(PASSES):
                nc.tensor.matmul_mx(
                    out=acc[:],
                    lhsT=ht_codes[:, g, rows].bitcast(FP8X4),
                    lhsT_scale=ht_scales[:, g, rows],
                    rhs=codes_of[parts[g]],
                    rhs_scale=scales_of[parts[g]],
                    start=(g == 0),
                    stop=(g == PASSES - 1),
                )
            nc.scalar.activation(out=y, in_=acc[:], func=ACT.Sigmoid)

        transpose(0)
        for i in range(B_TILES):
            tanh_tile(i)
        quantise_act(0)
        regroup(0)
        keep_clock(7, 4)
        transpose(1)
        quantise(0)
        transpose(2)
        quantise_act(1)
        gate_passes(0, [0])
        regroup_first(1)
        quantise_act(2)
        regroup_second(1)
        gate_passes(0, [1])
        for j in range(2, GATE_CHUNKS):
            regroup(j)
            quantise(j - 1)
            gate_passes(j - 1)
        quantise(GATE_CHUNKS - 1)
        gate_passes(GATE_CHUNKS - 1)

        first = GATE_CHUNKS
        regroup(first)
        regroup_first(first + 1)
        regroup_vector(first + 1)
        for i in range(B_TILES):
            hidden_state(0, i)
        quantise(first)
        for i in range(B_TILES):
            hidden_state(1, i)
        regroup_scalar(first + 1)
        transpose_hidden_state(0)
        transpose_hidden_state(1)
        keep_clock(0, 3)
        quantise(first + 1)
        quantise_hidden_state(0)
        regroup_first(first + 2)
        quantise_hidden_state(1)
        nc.sync.dma_start(out=ht_rows, in_=tanh_c[:])
        regroup_second(first + 2)
        regroup_scalar(first + 3)
        readout_passes([0, 1])
        regroup_first(first + 3)
        quantise(first + 2)
        regroup_vector(first + 3)
        keep_clock(0, 3)
        for n in range(2, N_BLOCKS + 1):
            ahead = n + 2 < N_BLOCKS + 1
            if ahead:
                regroup_scalar(first + n + 2)
            if n < N_BLOCKS - 1:
                readout_passes([n])
            else:
                readout_last(n - N_BLOCKS + 1)
            if ahead:
                regroup_first(first + n + 2)
            if n < N_BLOCKS:
                quantise(first + n + 1)
            if ahead:
                regroup_vector(first + n + 2)
